import numpy as np
import ml_dtypes


def mxq(x, axis, fmt="e4m3"):
    dtype, down = {"e4m3": (ml_dtypes.float8_e4m3fn, 7), "e5m2": (ml_dtypes.float8_e5m2, 14)}[fmt]
    v = np.moveaxis(np.asarray(x, np.float32).astype(ml_dtypes.bfloat16).astype(np.float64), axis, -1)
    blocks = v.reshape(v.shape[:-1] + (-1, 32))
    amax = np.abs(blocks).max(-1, keepdims=True)
    byte = np.maximum(np.where(amax > 0, np.frexp(amax)[1] - 1 + 127, 0) - down, 1)
    scale = np.exp2(byte - 127.0)
    codes = (blocks / scale).astype(np.float32).astype(dtype).astype(np.float64)
    return np.moveaxis((codes * scale).reshape(v.shape), -1, axis)


WIDE = False


def mx_kscale(k):
    if not WIDE:
        return np.ones(k)
    levels = np.array([10, -10, 5, -5, 0])
    a = np.random.permutation(np.resize(levels, k // 512 * 4)).reshape(k // 512, 4)
    idx = np.arange(k)
    return np.exp2(a[idx // 512, idx % 128 // 32])


BF16 = ml_dtypes.bfloat16


def bf(x):
    return np.asarray(x, np.float32).astype(BF16)


def f64(x):
    return np.asarray(x).astype(np.float64)


B, S, HID, NH = 4, 1024, 512, 4
D = HID // NH
COS_EPS = 1e-8
D2_EPS = 1e-12
SW_BASE = np.array([0.0, 1.5, 0.5])


def setup_inputs():
    s = mx_kscale(HID)
    return {
        "q": bf(np.random.standard_normal((B, NH, S, D)) * 1.1),
        "k": bf(np.random.standard_normal((B, NH, S, D)) * 1.1),
        "value": bf(np.random.standard_normal((B, S, HID)) * s),
        "Wv": bf(np.random.standard_normal((HID, HID)) * 2.0 / np.sqrt(HID) / s[None, :]),
        "bv": bf(np.random.standard_normal(HID) * 0.1),
        "scoring_weights": bf(SW_BASE + 0.1 * np.random.standard_normal(SW_BASE.shape)),
    }


def reference(q, k, value, Wv, bv, scoring_weights):
    vp = (mxq(f64(value), 2, "e4m3") @ mxq(f64(Wv), 1, "e4m3").T) + f64(bv)
    v = vp.reshape(B, S, NH, D).transpose(0, 2, 1, 3)
    dot = f64(q) @ f64(k).transpose(0, 1, 3, 2)
    qn = np.sqrt((f64(q) ** 2).sum(-1))
    kn = np.sqrt((f64(k) ** 2).sum(-1))
    cos = dot / np.maximum(qn[..., :, None] * kn[..., None, :], COS_EPS)
    d2 = qn[..., :, None] ** 2 + kn[..., None, :] ** 2 - 2.0 * dot
    euc = -np.sqrt(np.maximum(d2, D2_EPS))
    sw = f64(scoring_weights)
    w = np.exp(sw - sw.max())
    w = w / w.sum()
    scores = w[0] * dot + w[1] * cos + w[2] * euc
    e = np.exp(scores - scores.max(-1, keepdims=True))
    ctx = (mxq(e, 3, "e4m3") @ mxq(v, 2, "e4m3")) / e.sum(-1, keepdims=True)
    return ctx.transpose(0, 2, 1, 3).reshape(B, S, HID)

@@ -1,0 +1,459 @@
+from contextlib import ExitStack
+
+import concourse.mybir as mybir
+from concourse.masks import make_identity
+
+F32 = mybir.dt.float32
+BF16 = mybir.dt.bfloat16
+U32 = mybir.dt.uint32
+U8 = mybir.dt.uint8
+FP8X4 = mybir.dt.float8_e4m3fn_x4
+ALU = mybir.AluOpType
+ACT = mybir.ActivationFunctionType
+
+P = 128
+B, NH, S, D = 4, 4, 1024, 128
+HID = NH * D
+HEADS = B * NH
+TILES = S // P
+BANK = 512
+HALVES = S // BANK
+PACK = 4
+K_PASS = P * PACK
+PASSES = S // K_PASS
+D2_EPS = 1e-12
+NORM2_MIN = 1e-20
+W1_MIN = 1e-12
+FLOPS = 2 * (B * S * HID * HID + 2 * HEADS * S * S * D)
+
+
+def tile_adaptiveattention_pa_t_kernel(tc, q, k, value, Wv, bv, scoring_weights, out):
+    nc = tc.nc
+    with ExitStack() as ctx:
+        const = ctx.enter_context(tc.tile_pool(name="const", bufs=1))
+        vkeep = ctx.enter_context(tc.tile_pool(name="vkeep", bufs=1))
+        vwork = ctx.enter_context(tc.tile_pool(name="vwork", bufs=2))
+        nat = ctx.enter_context(tc.tile_pool(name="nat", bufs=2))
+        turned = ctx.enter_context(tc.tile_pool(name="turned", bufs=2))
+        squares = ctx.enter_context(tc.tile_pool(name="squares", bufs=1))
+        terms = ctx.enter_context(tc.tile_pool(name="terms", bufs=3))
+        spread = ctx.enter_context(tc.tile_pool(name="spread", bufs=1))
+        dist = ctx.enter_context(tc.tile_pool(name="dist", bufs=TILES))
+        score = ctx.enter_context(tc.tile_pool(name="score", bufs=TILES + 2))
+        soft = ctx.enter_context(tc.tile_pool(name="soft", bufs=4))
+        result = ctx.enter_context(tc.tile_pool(name="result", bufs=2))
+        banks = ctx.enter_context(tc.psum_pool(name="banks", bufs=4))
+        flipped = ctx.enter_context(tc.psum_pool(name="flipped", bufs=2))
+        context = ctx.enter_context(tc.psum_pool(name="context", bufs=2))
+        ctx.enter_context(tc.manual_schedule())
+
+        ident_bf = const.tile([P, P], BF16, name="ident_bf")
+        make_identity(nc, ident_bf[:])
+        ident_f32 = const.tile([P, P], F32, name="ident_f32")
+        make_identity(nc, ident_f32[:])
+        ones = const.tile([P, 2], F32, name="ones")
+        nc.vector.memset(ones[:], 1.0)
+        sw_all = const.tile([P, 3], BF16, name="sw_all")
+        nc.sync.dma_start(out=sw_all[:], in_=scoring_weights.partition_broadcast(P))
+        bv_all = const.tile([P, HID], BF16, name="bv_all")
+        nc.sync.dma_start(out=bv_all[:], in_=bv.partition_broadcast(P))
+
+        head = {}
+
+        def load_head(m):
+            b, h = divmod(m, NH)
+            q_nat = nat.tile([P, TILES, D], BF16, name="q_nat", tag="q_nat")
+            nc.sync.dma_start(out=q_nat[:], in_=q[b, h].rearrange("(p t) d -> p t d", t=TILES))
+            k_nat = nat.tile([P, TILES, D], BF16, name="k_nat", tag="k_nat")
+            nc.sync.dma_start(out=k_nat[:], in_=k[b, h].rearrange("(t p) d -> p t d", p=P))
+            head[m] = {"q_nat": q_nat, "k_nat": k_nat}
+
+        load_head(0)
+        w_nat = vkeep.tile([P, NH, HID], BF16, name="w_nat")
+        nc.sync.dma_start(out=w_nat[:], in_=Wv.rearrange("(t p) c -> p t c", p=P))
+
+        def load_value(b):
+            x_nat = vwork.tile([P, PASSES * PACK, HID], BF16, name="x_nat", tag="x_nat")
+            nc.sync.dma_start(
+                out=x_nat[:].rearrange("p (a e) c -> p a (e c)", e=2),
+                in_=value[b].rearrange("(a p e) c -> p a (e c)", p=P, e=2),
+            )
+            return x_nat
+
+        x_nats = {0: load_value(0)}
+        load_head(1)
+        x_nats[1] = load_value(1)
+
+        sw = const.tile([P, 3], F32, name="sw")
+        nc.vector.tensor_copy(out=sw[:], in_=sw_all[:])
+        sw_max = const.tile([P, 1], F32, name="sw_max")
+        nc.vector.tensor_reduce(out=sw_max[:], in_=sw[:], axis=mybir.AxisListType.X, op=ALU.max)
+        sw_shift = const.tile([P, 1], F32, name="sw_shift")
+        nc.vector.tensor_scalar_mul(out=sw_shift[:], in0=sw_max[:], scalar1=-1.0)
+        sw_exp = const.tile([P, 3], F32, name="sw_exp")
+        sw_sum = const.tile([P, 1], F32, name="sw_sum")
+        nc.scalar.activation(out=sw_exp[:], in_=sw[:], func=ACT.Exp, bias=sw_shift[:], accum_out=sw_sum[:])
+        sw_inv = const.tile([P, 1], F32, name="sw_inv")
+        nc.vector.reciprocal(out=sw_inv[:], in_=sw_sum[:])
+        w_mix = const.tile([P, 3], F32, name="w_mix")
+        nc.vector.tensor_scalar_mul(out=w_mix[:], in0=sw_exp[:], scalar1=sw_inv[:])
+        w1 = const.tile([P, 1], F32, name="w1")
+        nc.vector.tensor_scalar_max(out=w1[:], in0=w_mix[:, 1:2], scalar1=W1_MIN)
+        w1_inv = const.tile([P, 1], F32, name="w1_inv")
+        nc.vector.reciprocal(out=w1_inv[:], in_=w1[:])
+        w0_over_w1 = const.tile([P, 1], F32, name="w0_over_w1")
+        nc.vector.tensor_mul(out=w0_over_w1[:], in0=w_mix[:, 0:1], in1=w1_inv[:])
+        w2_over_w1 = const.tile([P, 1], F32, name="w2_over_w1")
+        nc.vector.tensor_mul(out=w2_over_w1[:], in0=w_mix[:, 2:3], in1=w1_inv[:])
+
+        def turn_features(rows, n_tiles, grouped):
+            words = rows.bitcast(F32)
+            grouped_words = grouped.bitcast(F32).rearrange("p (a r u) -> p a r u", r=P, u=2)
+            for pair in range(n_tiles // 2):
+                bank = banks.tile([P, 2, 2, P], F32, name="feat", tag="bank")
+                for a in range(2):
+                    for u in range(2):
+                        nc.tensor.transpose(
+                            bank[:, a, u, :], words[:, 2 * pair + a, u * P : (u + 1) * P], ident_f32[:]
+                        )
+                nc.scalar.copy(
+                    out=grouped_words[:, 2 * pair : 2 * pair + 2, :, :],
+                    in_=bank[:].rearrange("p a u r -> p a r u"),
+                )
+
+        w_grouped = vkeep.tile([P, NH * P * PACK], BF16, name="w_grouped", align_bytes=64)
+        turn_features(w_nat[:], NH, w_grouped[:])
+        w_codes = vkeep.tile([P, HID], U32, name="w_codes", align_bytes=64)
+        w_scales = vkeep.tile([P, HID], U8, name="w_scales", align_bytes=64)
+        nc.vector.quantize_mx(out=w_codes[:].bitcast(FP8X4), scales=w_scales[:], in_=w_grouped[:])
+
+        v_codes = {}
+        v_scales = {}
+        x_grouped = {}
+
+        def turn_value(b):
+            x_grouped[b] = vwork.tile(
+                [P, PASSES * PACK * P * PACK], BF16, name="x_grouped", tag="x_grouped", align_bytes=64
+            )
+            turn_features(x_nats[b][:], PASSES * PACK, x_grouped[b][:])
+
+        def project_value(b):
+            x_codes = vwork.tile([P, PASSES * PACK * P], U32, name="x_codes", tag="x_codes", align_bytes=64)
+            x_scales = vwork.tile([P, PASSES * PACK * P], U8, name="x_scales", tag="x_scales", align_bytes=64)
+            nc.vector.quantize_mx(out=x_codes[:].bitcast(FP8X4), scales=x_scales[:], in_=x_grouped[b][:])
+            v_codes[b] = vkeep.tile([P, PASSES, HID], U32, name="v_codes%d" % b, align_bytes=64)
+            v_scales[b] = vkeep.tile([P, PASSES, HID], U8, name="v_scales%d" % b, align_bytes=64)
+            for g in range(PASSES):
+                v_grouped = vwork.tile([P, NH, D, PACK], BF16, name="v_grouped", tag="v_grouped", align_bytes=64)
+                for h in range(NH):
+                    vp = banks.tile([P, PACK, D], F32, name="vp", tag="bank")
+                    for t in range(PACK):
+                        rows = slice((g * PACK + t) * P, (g * PACK + t + 1) * P)
+                        nc.tensor.matmul_mx(
+                            out=vp[:, t, :],
+                            lhsT=x_codes[:, rows].bitcast(FP8X4),
+                            lhsT_scale=x_scales[:, rows],
+                            rhs=w_codes[:, h * D : (h + 1) * D].bitcast(FP8X4),
+                            rhs_scale=w_scales[:, h * D : (h + 1) * D],
+                            start=True,
+                            stop=True,
+                        )
+                    nc.vector.tensor_tensor(
+                        out=v_grouped[:, h, :, :],
+                        in0=vp[:].rearrange("p t d -> p d t"),
+                        in1=bv_all[:, h * D : (h + 1) * D].unsqueeze(2).to_broadcast([P, D, PACK]),
+                        op=ALU.add,
+                    )
+                nc.vector.quantize_mx(
+                    out=v_codes[b][:, g, :].bitcast(FP8X4),
+                    scales=v_scales[b][:, g, :],
+                    in_=v_grouped[:].rearrange("p h d t -> p (h d t)"),
+                )
+
+        def turn_head(m):
+            for name in ("q", "k"):
+                bank = banks.tile([P, S], BF16, name="turn", tag="bank")
+                for t in range(TILES):
+                    nc.tensor.transpose(bank[:, t * P : (t + 1) * P], head[m][name + "_nat"][:, t, :], ident_bf[:])
+                head[m][name + "T"] = turned.tile([P, S], BF16, name=name + "T", tag=name + "T")
+                nc.scalar.copy(out=head[m][name + "T"][:], in_=bank[:])
+
+        def square_head(m):
+            for name in ("q", "k"):
+                sq = squares.tile([P, S], F32, name=name + "_sq", tag=name + "_sq")
+                nc.gpsimd.tensor_tensor(out=sq[:], in0=head[m][name + "T"][:], in1=head[m][name + "T"][:], op=ALU.mult)
+                head[m][name + "_sq"] = sq
+
+        def sum_squares(m):
+            norm2 = banks.tile([P, 2 * TILES, 2], F32, name="norm2", tag="bank")
+            for n_op, name in enumerate(("q", "k")):
+                for t in range(TILES):
+                    nc.tensor.matmul(
+                        out=norm2[:, n_op * TILES + t, :],
+                        lhsT=head[m][name + "_sq"][:, t * P : (t + 1) * P],
+                        rhs=ones[:],
+                        start=True,
+                        stop=True,
+                    )
+            head[m]["norm2"] = norm2
+
+        def floor_norms(m):
+            t = head[m]
+            t["half"] = terms.tile([P, 2 * TILES], F32, name="half", tag="half")
+            nc.vector.tensor_scalar_mul(out=t["half"][:], in0=t["norm2"][:, :, 0], scalar1=0.5)
+            t["floored"] = terms.tile([P, 2 * TILES], F32, name="floored", tag="floored")
+            nc.vector.tensor_scalar_max(out=t["floored"][:], in0=t["norm2"][:, :, 0], scalar1=NORM2_MIN)
+
+        def root_norms(m):
+            t = head[m]
+            t["norm"] = terms.tile([P, 2 * TILES], F32, name="norm", tag="norm")
+            nc.scalar.activation(out=t["norm"][:], in_=t["floored"][:], func=ACT.Sqrt)
+
+        def row_terms(m):
+            t = head[m]
+            t["inv"] = terms.tile([P, 2 * TILES], F32, name="inv", tag="inv")
+            nc.vector.reciprocal(out=t["inv"][:], in_=t["norm"][:])
+            t["c"] = terms.tile([P, TILES], F32, name="c", tag="c")
+            nc.vector.tensor_scalar_mul(out=t["c"][:], in0=t["inv"][:, 0:TILES], scalar1=w1[:])
+            t["g"] = terms.tile([P, TILES], F32, name="g", tag="g")
+            nc.vector.tensor_scalar_mul(out=t["g"][:], in0=t["norm"][:, 0:TILES], scalar1=w0_over_w1[:])
+            far = terms.tile([P, TILES], F32, name="far", tag="far")
+            nc.vector.tensor_scalar_mul(out=far[:], in0=t["norm"][:, 0:TILES], scalar1=w2_over_w1[:])
+            t["root_scale"] = terms.tile([P, TILES], F32, name="root_scale", tag="root_scale")
+            nc.vector.scalar_tensor_tensor(
+                out=t["root_scale"][:], in0=far[:], scalar=-2.0, in1=far[:], op0=ALU.mult, op1=ALU.mult
+            )
+
+        def spread_key_terms(m):
+            t = head[m]
+            t["spread_banks"] = []
+            for source in ("half", "inv"):
+                for half in range(HALVES):
+                    bank = banks.tile([P, BANK], F32, name="spread", tag="bank")
+                    for c in range(BANK // P):
+                        col = TILES + half * (BANK // P) + c
+                        nc.tensor.transpose(
+                            bank[:, c * P : (c + 1) * P], t[source][:, col : col + 1].to_broadcast([P, P]), ident_f32[:]
+                        )
+                    t["spread_banks"].append(bank)
+
+        def keep_key_terms(m):
+            t = head[m]
+            t["k_half"] = spread.tile([P, S], F32, name="k_half", tag="k_half")
+            t["k_inv"] = spread.tile([P, S], F32, name="k_inv", tag="k_inv")
+            for n_src, name in enumerate(("k_half", "k_inv")):
+                for half in range(HALVES):
+                    nc.scalar.copy(
+                        out=t[name][:, half * BANK : (half + 1) * BANK], in_=t["spread_banks"][n_src * HALVES + half][:]
+                    )
+
+        def multiply_scores(m, s):
+            t = head[m]
+            t["dot", s] = []
+            for half in range(HALVES):
+                bank = banks.tile([P, BANK], F32, name="dot", tag="bank")
+                nc.tensor.matmul(
+                    out=bank[:],
+                    lhsT=t["qT"][:, s * P : (s + 1) * P],
+                    rhs=t["kT"][:, half * BANK : (half + 1) * BANK],
+                    start=True,
+                    stop=True,
+                )
+                t["dot", s].append(bank)
+
+        def distance_and_cosine(m, s):
+            t = head[m]
+            t["far", s] = dist.tile([P, S], F32, name="far_t", tag="far_t")
+            t["near", s] = score.tile([P, S], F32, name="near_t", tag="near_t")
+            for half in range(HALVES):
+                cols = slice(half * BANK, (half + 1) * BANK)
+                nc.vector.scalar_tensor_tensor(
+                    out=t["far", s][:, cols],
+                    in0=t["dot", s][half][:],
+                    scalar=t["half"][:, s : s + 1],
+                    in1=t["k_half"][:, cols],
+                    op0=ALU.subtract,
+                    op1=ALU.subtract,
+                )
+            for half in range(HALVES):
+                cols = slice(half * BANK, (half + 1) * BANK)
+                nc.vector.scalar_tensor_tensor(
+                    out=t["near", s][:, cols],
+                    in0=t["k_inv"][:, cols],
+                    scalar=t["g"][:, s : s + 1],
+                    in1=t["dot", s][half][:],
+                    op0=ALU.add,
+                    op1=ALU.mult,
+                )
+
+        def floor_distance(m, s):
+            far = head[m]["far", s]
+            nc.gpsimd.tensor_scalar(
+                out=far[:], in0=far[:], scalar1=-0.5 * D2_EPS, scalar2=-3.0e38, op0=ALU.min, op1=ALU.max
+            )
+
+        def root_distance(m, s):
+            t = head[m]
+            nc.scalar.activation(
+                out=t["far", s][:], in_=t["far", s][:], func=ACT.Sqrt, scale=t["root_scale"][:, s : s + 1]
+            )
+
+        def mix(m, s):
+            t = head[m]
+            engine = nc.vector if s % 2 == 0 else nc.gpsimd
+            engine.tensor_tensor(out=t["near", s][:], in0=t["near", s][:], in1=t["far", s][:], op=ALU.subtract)
+
+        def row_maximum(m, s):
+            t = head[m]
+            nc.vector.tensor_reduce(
+                out=t["z_max"][:, s : s + 1], in_=t["near", s][:], axis=mybir.AxisListType.X, op=ALU.max
+            )
+
+        def exponential(m, s):
+            t = head[m]
+            t["e", s] = soft.tile([P, S], BF16, name="e", tag="e")
+            nc.scalar.activation(
+                out=t["e", s][:],
+                in_=t["near", s][:],
+                func=ACT.Exp,
+                bias=t["shift"][:, s : s + 1],
+                scale=t["c"][:, s : s + 1],
+                accum_out=t["row_sum"][:, s : s + 1],
+            )
+
+        def turn_weights(m, s):
+            t = head[m]
+            t["eT", s] = flipped.tile([P, PASSES * 2, P], F32, name="eT", tag="eT")
+            words = t["e", s][:].bitcast(F32)
+            for a in range(PASSES * 2):
+                nc.tensor.transpose(t["eT", s][:, a, :], words[:, a * P : (a + 1) * P], ident_f32[:])
+
+        def group_weights(m, s):
+            t = head[m]
+            t["e_grouped", s] = soft.tile([P, S], BF16, name="e_grouped", tag="e_grouped", align_bytes=64)
+            nc.scalar.copy(
+                out=t["e_grouped", s][:].bitcast(F32).rearrange("p (g i u) -> p g i u", g=PASSES, u=2),
+                in_=t["eT", s][:].rearrange("p (g u) i -> p g i u", u=2),
+            )
+
+        def quantise_weights(m, s):
+            t = head[m]
+            t["e_codes", s] = soft.tile([P, PASSES * P], U32, name="e_codes", tag="e_codes", align_bytes=64)
+            t["e_scales", s] = soft.tile([P, PASSES * P], U8, name="e_scales", tag="e_scales", align_bytes=64)
+            nc.vector.quantize_mx(
+                out=t["e_codes", s][:].bitcast(FP8X4), scales=t["e_scales", s][:], in_=t["e_grouped", s][:]
+            )
+
+        def multiply_context(m, s):
+            t = head[m]
+            b, h = divmod(m, NH)
+            per_bank = BANK // D
+            if s % per_bank == 0:
+                t["ctx", s // per_bank] = context.tile([P, per_bank, D], F32, name="ctx", tag="ctx")
+            for g in range(PASSES):
+                nc.tensor.matmul_mx(
+                    out=t["ctx", s // per_bank][:, s % per_bank, :],
+                    lhsT=t["e_codes", s][:, g * P : (g + 1) * P].bitcast(FP8X4),
+                    lhsT_scale=t["e_scales", s][:, g * P : (g + 1) * P],
+                    rhs=v_codes[b][:, g, h * D : (h + 1) * D].bitcast(FP8X4),
+                    rhs_scale=v_scales[b][:, g, h * D : (h + 1) * D],
+                    start=(g == 0),
+                    stop=(g == PASSES - 1),
+                )
+
+        def write_out(m):
+            t = head[m]
+            b, h = divmod(m, NH)
+            per_bank = BANK // D
+            sum_inv = result.tile([P, TILES], F32, name="sum_inv", tag="sum_inv")
+            nc.vector.reciprocal(out=sum_inv[:], in_=t["row_sum"][:])
+            o_sb = result.tile([P, TILES, D], F32, name="o_sb", tag="o_sb")
+            for n_bank in range(TILES // per_bank):
+                tiles = slice(n_bank * per_bank, (n_bank + 1) * per_bank)
+                nc.vector.tensor_tensor(
+                    out=o_sb[:, tiles, :],
+                    in0=t["ctx", n_bank][:],
+                    in1=sum_inv[:, tiles].unsqueeze(2).to_broadcast([P, per_bank, D]),
+                    op=ALU.mult,
+                )
+            nc.sync.dma_start(
+                out=out[b].rearrange("(p t) c -> p t c", t=TILES)[:, :, h * D : (h + 1) * D], in_=o_sb[:]
+            )
+
+        def part_a(m):
+            nxt = m + 1
+            if m + 4 < HEADS:
+                load_head(m + 4)
+            if nxt + 1 < HEADS:
+                square_head(nxt + 1)
+            if m >= 0:
+                head[m]["row_sum"] = result.tile([P, TILES], F32, name="row_sum", tag="row_sum")
+            for s in range(TILES + 2):
+                if nxt < HEADS and s < TILES:
+                    if s + 1 < TILES:
+                        multiply_scores(nxt, s + 1)
+                    distance_and_cosine(nxt, s)
+                    floor_distance(nxt, s)
+                if m >= 0:
+                    if s < TILES:
+                        exponential(m, s)
+                        turn_weights(m, s)
+                    if 1 <= s <= TILES:
+                        group_weights(m, s - 1)
+                    if s >= 2:
+                        quantise_weights(m, s - 2)
+                        multiply_context(m, s - 2)
+            if nxt + 1 < HEADS:
+                sum_squares(nxt + 1)
+
+        def part_b(m):
+            nxt = m + 1
+            if nxt + 1 < HEADS:
+                floor_norms(nxt + 1)
+                root_norms(nxt + 1)
+            if m >= 0:
+                write_out(m)
+            if nxt + 1 < HEADS:
+                row_terms(nxt + 1)
+                spread_key_terms(nxt + 1)
+            if nxt < HEADS:
+                t = head[nxt]
+                t["z_max"] = result.tile([P, TILES], F32, name="z_max", tag="z_max")
+                for s in range(TILES + 1):
+                    if s < TILES:
+                        root_distance(nxt, s)
+                        mix(nxt, s)
+                    if s >= 1:
+                        row_maximum(nxt, s - 1)
+                t["shift"] = result.tile([P, TILES], F32, name="shift", tag="shift")
+                nc.vector.scalar_tensor_tensor(
+                    out=t["shift"][:], in0=t["z_max"][:], scalar=-1.0, in1=t["c"][:], op0=ALU.mult, op1=ALU.mult
+                )
+            if nxt + 1 < HEADS:
+                keep_key_terms(nxt + 1)
+            if nxt + 2 < HEADS:
+                turn_head(nxt + 2)
+            if nxt + 1 < HEADS:
+                multiply_scores(nxt + 1, 0)
+
+        turn_head(0)
+        square_head(0)
+        turn_value(0)
+        sum_squares(0)
+        floor_norms(0)
+        root_norms(0)
+        row_terms(0)
+        spread_key_terms(0)
+        keep_key_terms(0)
+        turn_head(1)
+        load_head(2)
+        for b in range(B):
+            if b + 1 < B:
+                turn_value(b + 1)
+            project_value(b)
+            if b + 2 < B:
+                x_nats[b + 2] = load_value(b + 2)
+        multiply_scores(0, 0)
+        for m in range(-1, HEADS):
+            part_a(m)
+            part_b(m)

@@ -34,9 +34,9 @@ def tile_adaptiveattention_pa_t_kernel(tc, q, k, value, Wv, bv, scoring_weights,
         vkeep = ctx.enter_context(tc.tile_pool(name="vkeep", bufs=1))
         vwork = ctx.enter_context(tc.tile_pool(name="vwork", bufs=2))
         nat = ctx.enter_context(tc.tile_pool(name="nat", bufs=2))
-        turned = ctx.enter_context(tc.tile_pool(name="turned", bufs=2))
+        turned = ctx.enter_context(tc.tile_pool(name="turned", bufs=3))
         squares = ctx.enter_context(tc.tile_pool(name="squares", bufs=1))
-        terms = ctx.enter_context(tc.tile_pool(name="terms", bufs=3))
+        terms = ctx.enter_context(tc.tile_pool(name="terms", bufs=5))
         spread = ctx.enter_context(tc.tile_pool(name="spread", bufs=1))
         dist = ctx.enter_context(tc.tile_pool(name="dist", bufs=TILES))
         score = ctx.enter_context(tc.tile_pool(name="score", bufs=TILES + 2))
@@ -170,13 +170,12 @@ def tile_adaptiveattention_pa_t_kernel(tc, q, k, value, Wv, bv, scoring_weights,
                     in_=v_grouped[:].rearrange("p h d t -> p (h d t)"),
                 )
 
-        def turn_head(m):
-            for name in ("q", "k"):
-                bank = banks.tile([P, S], BF16, name="turn", tag="bank")
-                for t in range(TILES):
-                    nc.tensor.transpose(bank[:, t * P : (t + 1) * P], head[m][name + "_nat"][:, t, :], ident_bf[:])
-                head[m][name + "T"] = turned.tile([P, S], BF16, name=name + "T", tag=name + "T")
-                nc.scalar.copy(out=head[m][name + "T"][:], in_=bank[:])
+        def turn_head(m, name):
+            bank = banks.tile([P, S], BF16, name="turn", tag="bank")
+            for t in range(TILES):
+                nc.tensor.transpose(bank[:, t * P : (t + 1) * P], head[m][name + "_nat"][:, t, :], ident_bf[:])
+            head[m][name + "T"] = turned.tile([P, S], BF16, name=name + "T", tag=name + "T")
+            nc.scalar.copy(out=head[m][name + "T"][:], in_=bank[:])
 
         def square_head(m):
             for name in ("q", "k"):
@@ -185,7 +184,7 @@ def tile_adaptiveattention_pa_t_kernel(tc, q, k, value, Wv, bv, scoring_weights,
                 head[m][name + "_sq"] = sq
 
         def sum_squares(m):
-            norm2 = banks.tile([P, 2 * TILES, 2], F32, name="norm2", tag="bank")
+            norm2 = flipped.tile([P, 2 * TILES, 2], F32, name="norm2", tag="eT")
             for n_op, name in enumerate(("q", "k")):
                 for t in range(TILES):
                     nc.tensor.matmul(
@@ -237,15 +236,14 @@ def tile_adaptiveattention_pa_t_kernel(tc, q, k, value, Wv, bv, scoring_weights,
                         )
                     t["spread_banks"].append(bank)
 
-        def keep_key_terms(m):
+        def keep_key_terms(m, n_bank):
             t = head[m]
-            t["k_half"] = spread.tile([P, S], F32, name="k_half", tag="k_half")
-            t["k_inv"] = spread.tile([P, S], F32, name="k_inv", tag="k_inv")
-            for n_src, name in enumerate(("k_half", "k_inv")):
-                for half in range(HALVES):
-                    nc.scalar.copy(
-                        out=t[name][:, half * BANK : (half + 1) * BANK], in_=t["spread_banks"][n_src * HALVES + half][:]
-                    )
+            if n_bank == 0:
+                t["k_half"] = spread.tile([P, S], F32, name="k_half", tag="k_half")
+                t["k_inv"] = spread.tile([P, S], F32, name="k_inv", tag="k_inv")
+            name = ("k_half", "k_inv")[n_bank // HALVES]
+            half = n_bank % HALVES
+            nc.scalar.copy(out=t[name][:, half * BANK : (half + 1) * BANK], in_=t["spread_banks"][n_bank][:])
 
         def multiply_scores(m, s):
             t = head[m]
@@ -288,9 +286,7 @@ def tile_adaptiveattention_pa_t_kernel(tc, q, k, value, Wv, bv, scoring_weights,
 
         def floor_distance(m, s):
             far = head[m]["far", s]
-            nc.gpsimd.tensor_scalar(
-                out=far[:], in0=far[:], scalar1=-0.5 * D2_EPS, scalar2=-3.0e38, op0=ALU.min, op1=ALU.max
-            )
+            nc.vector.tensor_scalar_min(out=far[:], in0=far[:], scalar1=-0.5 * D2_EPS)
 
         def root_distance(m, s):
             t = head[m]
@@ -300,7 +296,7 @@ def tile_adaptiveattention_pa_t_kernel(tc, q, k, value, Wv, bv, scoring_weights,
 
         def mix(m, s):
             t = head[m]
-            engine = nc.vector if s % 2 == 0 else nc.gpsimd
+            engine = nc.gpsimd if s < TILES - 1 else nc.vector
             engine.tensor_tensor(out=t["near", s][:], in0=t["near", s][:], in1=t["far", s][:], op=ALU.subtract)
 
         def row_maximum(m, s):
@@ -382,10 +378,10 @@ def tile_adaptiveattention_pa_t_kernel(tc, q, k, value, Wv, bv, scoring_weights,
 
         def part_a(m):
             nxt = m + 1
-            if m + 4 < HEADS:
-                load_head(m + 4)
-            if nxt + 1 < HEADS:
-                square_head(nxt + 1)
+            if m + 5 < HEADS:
+                load_head(m + 5)
+            if m + 3 < HEADS:
+                square_head(m + 3)
             if m >= 0:
                 head[m]["row_sum"] = result.tile([P, TILES], F32, name="row_sum", tag="row_sum")
             for s in range(TILES + 2):
@@ -403,50 +399,59 @@ def tile_adaptiveattention_pa_t_kernel(tc, q, k, value, Wv, bv, scoring_weights,
                     if s >= 2:
                         quantise_weights(m, s - 2)
                         multiply_context(m, s - 2)
-            if nxt + 1 < HEADS:
-                sum_squares(nxt + 1)
 
         def part_b(m):
             nxt = m + 1
-            if nxt + 1 < HEADS:
-                floor_norms(nxt + 1)
-                root_norms(nxt + 1)
             if m >= 0:
                 write_out(m)
-            if nxt + 1 < HEADS:
-                row_terms(nxt + 1)
-                spread_key_terms(nxt + 1)
+            if m + 2 < HEADS:
+                row_terms(m + 2)
+                spread_key_terms(m + 2)
+            if m + 3 < HEADS:
+                sum_squares(m + 3)
             if nxt < HEADS:
-                t = head[nxt]
-                t["z_max"] = result.tile([P, TILES], F32, name="z_max", tag="z_max")
-                for s in range(TILES + 1):
+                head[nxt]["z_max"] = result.tile([P, TILES], F32, name="z_max", tag="z_max")
+            for s in range(TILES + 1):
+                if nxt < HEADS:
                     if s < TILES:
                         root_distance(nxt, s)
                         mix(nxt, s)
                     if s >= 1:
                         row_maximum(nxt, s - 1)
+                if 1 <= s <= 2 * HALVES and m + 2 < HEADS:
+                    keep_key_terms(m + 2, s - 1)
+                if s == 2 * HALVES + 1 and m + 4 < HEADS:
+                    turn_head(m + 4, "q")
+                if s == 2 * HALVES + 2 and m + 4 < HEADS:
+                    turn_head(m + 4, "k")
+            if nxt < HEADS:
+                t = head[nxt]
                 t["shift"] = result.tile([P, TILES], F32, name="shift", tag="shift")
                 nc.vector.scalar_tensor_tensor(
                     out=t["shift"][:], in0=t["z_max"][:], scalar=-1.0, in1=t["c"][:], op0=ALU.mult, op1=ALU.mult
                 )
-            if nxt + 1 < HEADS:
-                keep_key_terms(nxt + 1)
-            if nxt + 2 < HEADS:
-                turn_head(nxt + 2)
-            if nxt + 1 < HEADS:
-                multiply_scores(nxt + 1, 0)
+            if m + 3 < HEADS:
+                floor_norms(m + 3)
+                root_norms(m + 3)
+            if m + 2 < HEADS:
+                multiply_scores(m + 2, 0)
 
-        turn_head(0)
-        square_head(0)
+        for m in range(2):
+            turn_head(m, "q")
+            turn_head(m, "k")
+            square_head(m)
+            sum_squares(m)
+            floor_norms(m)
+            root_norms(m)
         turn_value(0)
-        sum_squares(0)
-        floor_norms(0)
-        root_norms(0)
         row_terms(0)
         spread_key_terms(0)
-        keep_key_terms(0)
-        turn_head(1)
+        for n_bank in range(2 * HALVES):
+            keep_key_terms(0, n_bank)
         load_head(2)
+        load_head(3)
+        turn_head(2, "q")
+        turn_head(2, "k")
         for b in range(B):
             if b + 1 < B:
                 turn_value(b + 1)

@@ -24,6 +24,7 @@ PASSES = S // K_PASS
 D2_EPS = 1e-12
 NORM2_MIN = 1e-20
 W1_MIN = 1e-12
+GPSIMD_TILES = 5
 FLOPS = 2 * (B * S * HID * HID + 2 * HEADS * S * S * D)
 
 
@@ -40,7 +41,7 @@ def tile_adaptiveattention_pa_t_kernel(tc, q, k, value, Wv, bv, scoring_weights,
         spread = ctx.enter_context(tc.tile_pool(name="spread", bufs=1))
         dist = ctx.enter_context(tc.tile_pool(name="dist", bufs=TILES))
         score = ctx.enter_context(tc.tile_pool(name="score", bufs=TILES + 2))
-        soft = ctx.enter_context(tc.tile_pool(name="soft", bufs=4))
+        soft = ctx.enter_context(tc.tile_pool(name="soft", bufs=3))
         result = ctx.enter_context(tc.tile_pool(name="result", bufs=2))
         banks = ctx.enter_context(tc.psum_pool(name="banks", bufs=4))
         flipped = ctx.enter_context(tc.psum_pool(name="flipped", bufs=2))
@@ -68,7 +69,6 @@ def tile_adaptiveattention_pa_t_kernel(tc, q, k, value, Wv, bv, scoring_weights,
             nc.sync.dma_start(out=k_nat[:], in_=k[b, h].rearrange("(t p) d -> p t d", p=P))
             head[m] = {"q_nat": q_nat, "k_nat": k_nat}
 
-        load_head(0)
         w_nat = vkeep.tile([P, NH, HID], BF16, name="w_nat")
         nc.sync.dma_start(out=w_nat[:], in_=Wv.rearrange("(t p) c -> p t c", p=P))
 
@@ -81,6 +81,7 @@ def tile_adaptiveattention_pa_t_kernel(tc, q, k, value, Wv, bv, scoring_weights,
             return x_nat
 
         x_nats = {0: load_value(0)}
+        load_head(0)
         load_head(1)
         x_nats[1] = load_value(1)
 
@@ -296,7 +297,7 @@ def tile_adaptiveattention_pa_t_kernel(tc, q, k, value, Wv, bv, scoring_weights,
 
         def mix(m, s):
             t = head[m]
-            engine = nc.gpsimd if s < TILES - 1 else nc.vector
+            engine = nc.gpsimd if s < GPSIMD_TILES else nc.vector
             engine.tensor_tensor(out=t["near", s][:], in0=t["near", s][:], in1=t["far", s][:], op=ALU.subtract)
 
         def row_maximum(m, s):
@@ -326,7 +327,7 @@ def tile_adaptiveattention_pa_t_kernel(tc, q, k, value, Wv, bv, scoring_weights,
 
         def group_weights(m, s):
             t = head[m]
-            t["e_grouped", s] = soft.tile([P, S], BF16, name="e_grouped", tag="e_grouped", align_bytes=64)
+            t["e_grouped", s] = soft.tile([P, S], BF16, name="e_grouped", tag="e_grouped", bufs=TILES, align_bytes=64)
             nc.scalar.copy(
                 out=t["e_grouped", s][:].bitcast(F32).rearrange("p (g i u) -> p g i u", g=PASSES, u=2),
                 in_=t["eT", s][:].rearrange("p (g u) i -> p g i u", u=2),
@@ -357,20 +358,22 @@ def tile_adaptiveattention_pa_t_kernel(tc, q, k, value, Wv, bv, scoring_weights,
                     stop=(g == PASSES - 1),
                 )
 
+        def invert_sums(m):
+            t = head[m]
+            t["sum_inv"] = result.tile([P, TILES], F32, name="sum_inv", tag="sum_inv")
+            nc.vector.reciprocal(out=t["sum_inv"][:], in_=t["row_sum"][:])
+
         def write_out(m):
             t = head[m]
             b, h = divmod(m, NH)
             per_bank = BANK // D
-            sum_inv = result.tile([P, TILES], F32, name="sum_inv", tag="sum_inv")
-            nc.vector.reciprocal(out=sum_inv[:], in_=t["row_sum"][:])
             o_sb = result.tile([P, TILES, D], F32, name="o_sb", tag="o_sb")
-            for n_bank in range(TILES // per_bank):
-                tiles = slice(n_bank * per_bank, (n_bank + 1) * per_bank)
-                nc.vector.tensor_tensor(
-                    out=o_sb[:, tiles, :],
-                    in0=t["ctx", n_bank][:],
-                    in1=sum_inv[:, tiles].unsqueeze(2).to_broadcast([P, per_bank, D]),
-                    op=ALU.mult,
+            for s in range(TILES):
+                nc.scalar.activation(
+                    out=o_sb[:, s, :],
+                    in_=t["ctx", s // per_bank][:, s % per_bank, :],
+                    func=ACT.Copy,
+                    scale=t["sum_inv"][:, s : s + 1],
                 )
             nc.sync.dma_start(
                 out=out[b].rearrange("(p t) c -> p t c", t=TILES)[:, :, h * D : (h + 1) * D], in_=o_sb[:]
@@ -391,73 +394,87 @@ def tile_adaptiveattention_pa_t_kernel(tc, q, k, value, Wv, bv, scoring_weights,
                     distance_and_cosine(nxt, s)
                     floor_distance(nxt, s)
                 if m >= 0:
-                    if s < TILES:
-                        exponential(m, s)
-                        turn_weights(m, s)
-                    if 1 <= s <= TILES:
-                        group_weights(m, s - 1)
+                    for w in range(2 * s, min(2 * s + 2, TILES)):
+                        exponential(m, w)
+                        turn_weights(m, w)
+                        if w >= 1:
+                            group_weights(m, w - 1)
+                    if 2 * s == TILES:
+                        group_weights(m, TILES - 1)
                     if s >= 2:
                         quantise_weights(m, s - 2)
                         multiply_context(m, s - 2)
+            if m + 3 < HEADS:
+                sum_squares(m + 3)
 
         def part_b(m):
             nxt = m + 1
             if m >= 0:
-                write_out(m)
+                invert_sums(m)
             if m + 2 < HEADS:
                 row_terms(m + 2)
                 spread_key_terms(m + 2)
-            if m + 3 < HEADS:
-                sum_squares(m + 3)
+            if nxt < HEADS:
+                for s in range(TILES):
+                    root_distance(nxt, s)
+                    if s < GPSIMD_TILES:
+                        mix(nxt, s)
+            if m >= 0:
+                write_out(m)
+            if m + 2 < HEADS:
+                for n_bank in range(2 * HALVES):
+                    keep_key_terms(m + 2, n_bank)
+            if m + 4 < HEADS:
+                turn_head(m + 4, "q")
+                turn_head(m + 4, "k")
             if nxt < HEADS:
                 head[nxt]["z_max"] = result.tile([P, TILES], F32, name="z_max", tag="z_max")
-            for s in range(TILES + 1):
-                if nxt < HEADS:
-                    if s < TILES:
-                        root_distance(nxt, s)
-                        mix(nxt, s)
-                    if s >= 1:
-                        row_maximum(nxt, s - 1)
-                if 1 <= s <= 2 * HALVES and m + 2 < HEADS:
-                    keep_key_terms(m + 2, s - 1)
-                if s == 2 * HALVES + 1 and m + 4 < HEADS:
-                    turn_head(m + 4, "q")
-                if s == 2 * HALVES + 2 and m + 4 < HEADS:
-                    turn_head(m + 4, "k")
+                for s in range(GPSIMD_TILES, TILES):
+                    mix(nxt, s)
+                    row_maximum(nxt, s)
+            if m + 3 < HEADS:
+                floor_norms(m + 3)
+                root_norms(m + 3)
             if nxt < HEADS:
+                for s in range(GPSIMD_TILES):
+                    row_maximum(nxt, s)
                 t = head[nxt]
                 t["shift"] = result.tile([P, TILES], F32, name="shift", tag="shift")
                 nc.vector.scalar_tensor_tensor(
                     out=t["shift"][:], in0=t["z_max"][:], scalar=-1.0, in1=t["c"][:], op0=ALU.mult, op1=ALU.mult
                 )
-            if m + 3 < HEADS:
-                floor_norms(m + 3)
-                root_norms(m + 3)
             if m + 2 < HEADS:
                 multiply_scores(m + 2, 0)
 
+        turn_value(0)
         for m in range(2):
             turn_head(m, "q")
             turn_head(m, "k")
-            square_head(m)
-            sum_squares(m)
-            floor_norms(m)
-            root_norms(m)
-        turn_value(0)
+        square_head(0)
+        turn_value(1)
+        project_value(0)
+        x_nats[2] = load_value(2)
+        sum_squares(0)
+        floor_norms(0)
+        root_norms(0)
+        square_head(1)
+        load_head(2)
+        load_head(3)
+        turn_value(2)
+        project_value(1)
+        x_nats[3] = load_value(3)
         row_terms(0)
         spread_key_terms(0)
         for n_bank in range(2 * HALVES):
             keep_key_terms(0, n_bank)
-        load_head(2)
-        load_head(3)
+        sum_squares(1)
+        floor_norms(1)
+        root_norms(1)
         turn_head(2, "q")
         turn_head(2, "k")
-        for b in range(B):
-            if b + 1 < B:
-                turn_value(b + 1)
-            project_value(b)
-            if b + 2 < B:
-                x_nats[b + 2] = load_value(b + 2)
+        turn_value(3)
+        project_value(2)
+        project_value(3)
         multiply_scores(0, 0)
         for m in range(-1, HEADS):
             part_a(m)

@@ -24,7 +24,15 @@ PASSES = S // K_PASS
 D2_EPS = 1e-12
 NORM2_MIN = 1e-20
 W1_MIN = 1e-12
-GPSIMD_TILES = 5
+FAR_MIN = -3.0e38
+QUAD = 4
+DIST_BUFS = 12
+SCORE_BUFS = 14
+ROOTS = ((0, 1, 2), (3, 4, 5), (6, 7), (), (), (), (), ())
+MIXES = ((0,), (1, 2), (3,), (4, 5), (6, 7), (), (), ())
+MAXIMA = ((), (0,), (1, 2), (3,), (4, 5), (6, 7), (), ())
+EXPONENTIALS = ((), (), (), (0,), (1, 2), (3, 4), (5, 6), (7,))
+FLOORS = ((), (), (), (), (), (0, 1, 2), (3, 4), (5, 6))
 FLOPS = 2 * (B * S * HID * HID + 2 * HEADS * S * S * D)
 
 
@@ -33,15 +41,12 @@ def tile_adaptiveattention_pa_t_kernel(tc, q, k, value, Wv, bv, scoring_weights,
     with ExitStack() as ctx:
         const = ctx.enter_context(tc.tile_pool(name="const", bufs=1))
         vkeep = ctx.enter_context(tc.tile_pool(name="vkeep", bufs=1))
-        vwork = ctx.enter_context(tc.tile_pool(name="vwork", bufs=2))
-        nat = ctx.enter_context(tc.tile_pool(name="nat", bufs=2))
+        nat = ctx.enter_context(tc.tile_pool(name="nat", bufs=3))
         turned = ctx.enter_context(tc.tile_pool(name="turned", bufs=3))
         squares = ctx.enter_context(tc.tile_pool(name="squares", bufs=1))
         terms = ctx.enter_context(tc.tile_pool(name="terms", bufs=5))
-        spread = ctx.enter_context(tc.tile_pool(name="spread", bufs=1))
-        dist = ctx.enter_context(tc.tile_pool(name="dist", bufs=TILES))
-        score = ctx.enter_context(tc.tile_pool(name="score", bufs=TILES + 2))
-        soft = ctx.enter_context(tc.tile_pool(name="soft", bufs=3))
+        spread = ctx.enter_context(tc.tile_pool(name="spread", bufs=2))
+        soft = ctx.enter_context(tc.tile_pool(name="soft", bufs=2))
         result = ctx.enter_context(tc.tile_pool(name="result", bufs=2))
         banks = ctx.enter_context(tc.psum_pool(name="banks", bufs=4))
         flipped = ctx.enter_context(tc.psum_pool(name="flipped", bufs=2))
@@ -69,9 +74,6 @@ def tile_adaptiveattention_pa_t_kernel(tc, q, k, value, Wv, bv, scoring_weights,
             nc.sync.dma_start(out=k_nat[:], in_=k[b, h].rearrange("(t p) d -> p t d", p=P))
             head[m] = {"q_nat": q_nat, "k_nat": k_nat}
 
-        w_nat = vkeep.tile([P, NH, HID], BF16, name="w_nat")
-        nc.sync.dma_start(out=w_nat[:], in_=Wv.rearrange("(t p) c -> p t c", p=P))
-
         def load_value(b):
             x_nat = vwork.tile([P, PASSES * PACK, HID], BF16, name="x_nat", tag="x_nat")
             nc.sync.dma_start(
@@ -79,11 +81,6 @@ def tile_adaptiveattention_pa_t_kernel(tc, q, k, value, Wv, bv, scoring_weights,
                 in_=value[b].rearrange("(a p e) c -> p a (e c)", p=P, e=2),
             )
             return x_nat
-
-        x_nats = {0: load_value(0)}
-        load_head(0)
-        load_head(1)
-        x_nats[1] = load_value(1)
 
         sw = const.tile([P, 3], F32, name="sw")
         nc.vector.tensor_copy(out=sw[:], in_=sw_all[:])
@@ -106,6 +103,10 @@ def tile_adaptiveattention_pa_t_kernel(tc, q, k, value, Wv, bv, scoring_weights,
         nc.vector.tensor_mul(out=w0_over_w1[:], in0=w_mix[:, 0:1], in1=w1_inv[:])
         w2_over_w1 = const.tile([P, 1], F32, name="w2_over_w1")
         nc.vector.tensor_mul(out=w2_over_w1[:], in0=w_mix[:, 2:3], in1=w1_inv[:])
+        root_factor = const.tile([P, 1], F32, name="root_factor")
+        nc.vector.scalar_tensor_tensor(
+            out=root_factor[:], in0=w2_over_w1[:], scalar=-2.0, in1=w2_over_w1[:], op0=ALU.mult, op1=ALU.mult
+        )
 
         def turn_features(rows, n_tiles, grouped):
             words = rows.bitcast(F32)
@@ -121,12 +122,6 @@ def tile_adaptiveattention_pa_t_kernel(tc, q, k, value, Wv, bv, scoring_weights,
                     out=grouped_words[:, 2 * pair : 2 * pair + 2, :, :],
                     in_=bank[:].rearrange("p a u r -> p a r u"),
                 )
-
-        w_grouped = vkeep.tile([P, NH * P * PACK], BF16, name="w_grouped", align_bytes=64)
-        turn_features(w_nat[:], NH, w_grouped[:])
-        w_codes = vkeep.tile([P, HID], U32, name="w_codes", align_bytes=64)
-        w_scales = vkeep.tile([P, HID], U8, name="w_scales", align_bytes=64)
-        nc.vector.quantize_mx(out=w_codes[:].bitcast(FP8X4), scales=w_scales[:], in_=w_grouped[:])
 
         v_codes = {}
         v_scales = {}
@@ -172,7 +167,7 @@ def tile_adaptiveattention_pa_t_kernel(tc, q, k, value, Wv, bv, scoring_weights,
                 )
 
         def turn_head(m, name):
-            bank = banks.tile([P, S], BF16, name="turn", tag="bank")
+            bank = flipped.tile([P, S], BF16, name="turn", tag="eT")
             for t in range(TILES):
                 nc.tensor.transpose(bank[:, t * P : (t + 1) * P], head[m][name + "_nat"][:, t, :], ident_bf[:])
             head[m][name + "T"] = turned.tile([P, S], BF16, name=name + "T", tag=name + "T")
@@ -209,42 +204,35 @@ def tile_adaptiveattention_pa_t_kernel(tc, q, k, value, Wv, bv, scoring_weights,
             t["norm"] = terms.tile([P, 2 * TILES], F32, name="norm", tag="norm")
             nc.scalar.activation(out=t["norm"][:], in_=t["floored"][:], func=ACT.Sqrt)
 
-        def row_terms(m):
+        def invert_norms(m):
             t = head[m]
             t["inv"] = terms.tile([P, 2 * TILES], F32, name="inv", tag="inv")
             nc.vector.reciprocal(out=t["inv"][:], in_=t["norm"][:])
-            t["c"] = terms.tile([P, TILES], F32, name="c", tag="c")
-            nc.vector.tensor_scalar_mul(out=t["c"][:], in0=t["inv"][:, 0:TILES], scalar1=w1[:])
-            t["g"] = terms.tile([P, TILES], F32, name="g", tag="g")
-            nc.vector.tensor_scalar_mul(out=t["g"][:], in0=t["norm"][:, 0:TILES], scalar1=w0_over_w1[:])
-            far = terms.tile([P, TILES], F32, name="far", tag="far")
-            nc.vector.tensor_scalar_mul(out=far[:], in0=t["norm"][:, 0:TILES], scalar1=w2_over_w1[:])
-            t["root_scale"] = terms.tile([P, TILES], F32, name="root_scale", tag="root_scale")
-            nc.vector.scalar_tensor_tensor(
-                out=t["root_scale"][:], in0=far[:], scalar=-2.0, in1=far[:], op0=ALU.mult, op1=ALU.mult
-            )
+
+        def row_terms(m):
+            t = head[m]
+            for name, source, factor in (
+                ("c", "inv", w1),
+                ("g", "norm", w0_over_w1),
+                ("root_scale", "floored", root_factor),
+            ):
+                t[name] = terms.tile([P, TILES], F32, name=name, tag=name)
+                nc.gpsimd.tensor_scalar(
+                    out=t[name][:], in0=t[source][:, 0:TILES], scalar1=factor[:], scalar2=1.0, op0=ALU.mult, op1=ALU.mult
+                )
 
         def spread_key_terms(m):
             t = head[m]
-            t["spread_banks"] = []
-            for source in ("half", "inv"):
+            for name, source in (("k_half", "half"), ("k_inv", "inv")):
+                t[name] = spread.tile([P, S], F32, name=name, tag=name)
                 for half in range(HALVES):
-                    bank = banks.tile([P, BANK], F32, name="spread", tag="bank")
+                    bank = flipped.tile([P, BANK], F32, name="spread", tag="eT")
                     for c in range(BANK // P):
                         col = TILES + half * (BANK // P) + c
                         nc.tensor.transpose(
                             bank[:, c * P : (c + 1) * P], t[source][:, col : col + 1].to_broadcast([P, P]), ident_f32[:]
                         )
-                    t["spread_banks"].append(bank)
-
-        def keep_key_terms(m, n_bank):
-            t = head[m]
-            if n_bank == 0:
-                t["k_half"] = spread.tile([P, S], F32, name="k_half", tag="k_half")
-                t["k_inv"] = spread.tile([P, S], F32, name="k_inv", tag="k_inv")
-            name = ("k_half", "k_inv")[n_bank // HALVES]
-            half = n_bank % HALVES
-            nc.scalar.copy(out=t[name][:, half * BANK : (half + 1) * BANK], in_=t["spread_banks"][n_bank][:])
+                    nc.scalar.copy(out=t[name][:, half * BANK : (half + 1) * BANK], in_=bank[:])
 
         def multiply_scores(m, s):
             t = head[m]
@@ -287,7 +275,9 @@ def tile_adaptiveattention_pa_t_kernel(tc, q, k, value, Wv, bv, scoring_weights,
 
         def floor_distance(m, s):
             far = head[m]["far", s]
-            nc.vector.tensor_scalar_min(out=far[:], in0=far[:], scalar1=-0.5 * D2_EPS)
+            nc.gpsimd.tensor_scalar(
+                out=far[:], in0=far[:], scalar1=-0.5 * D2_EPS, scalar2=FAR_MIN, op0=ALU.min, op1=ALU.max
+            )
 
         def root_distance(m, s):
             t = head[m]
@@ -297,18 +287,28 @@ def tile_adaptiveattention_pa_t_kernel(tc, q, k, value, Wv, bv, scoring_weights,
 
         def mix(m, s):
             t = head[m]
-            engine = nc.gpsimd if s < GPSIMD_TILES else nc.vector
-            engine.tensor_tensor(out=t["near", s][:], in0=t["near", s][:], in1=t["far", s][:], op=ALU.subtract)
+            nc.gpsimd.tensor_tensor(out=t["near", s][:], in0=t["near", s][:], in1=t["far", s][:], op=ALU.subtract)
 
         def row_maximum(m, s):
             t = head[m]
+            if s == 0:
+                t["z_max"] = result.tile([P, TILES], F32, name="z_max", tag="z_max")
             nc.vector.tensor_reduce(
-                out=t["z_max"][:, s : s + 1], in_=t["near", s][:], axis=mybir.AxisListType.X, op=ALU.max
+                out=t["z_max"][:, s : s + 1], in_=t["near", s][:], axis=mybir.AxisListType.X, op=ALU.max, negate=True
+            )
+
+        def shift_of(m, s):
+            t = head[m]
+            if s == 0:
+                t["shift"] = result.tile([P, TILES], F32, name="shift", tag="shift")
+                t["row_sum"] = result.tile([P, TILES], F32, name="row_sum", tag="row_sum")
+            nc.scalar.activation(
+                out=t["shift"][:, s : s + 1], in_=t["z_max"][:, s : s + 1], func=ACT.Copy, scale=t["c"][:, s : s + 1]
             )
 
         def exponential(m, s):
             t = head[m]
-            t["e", s] = soft.tile([P, S], BF16, name="e", tag="e")
+            t["e", s] = soft.tile([P, S], BF16, name="e", tag="e", bufs=3)
             nc.scalar.activation(
                 out=t["e", s][:],
                 in_=t["near", s][:],
@@ -327,36 +327,40 @@ def tile_adaptiveattention_pa_t_kernel(tc, q, k, value, Wv, bv, scoring_weights,
 
         def group_weights(m, s):
             t = head[m]
-            t["e_grouped", s] = soft.tile([P, S], BF16, name="e_grouped", tag="e_grouped", bufs=TILES, align_bytes=64)
+            quad, r = divmod(s, QUAD)
+            if r == 0:
+                t["e_grouped", quad] = soft.tile([P, QUAD, S], BF16, name="e_grouped", tag="e_grouped", align_bytes=64)
             nc.scalar.copy(
-                out=t["e_grouped", s][:].bitcast(F32).rearrange("p (g i u) -> p g i u", g=PASSES, u=2),
+                out=t["e_grouped", quad][:, r, :].bitcast(F32).rearrange("p (g i u) -> p g i u", g=PASSES, u=2),
                 in_=t["eT", s][:].rearrange("p (g u) i -> p g i u", u=2),
             )
 
-        def quantise_weights(m, s):
+        def quantise_weights(m, quad):
             t = head[m]
-            t["e_codes", s] = soft.tile([P, PASSES * P], U32, name="e_codes", tag="e_codes", align_bytes=64)
-            t["e_scales", s] = soft.tile([P, PASSES * P], U8, name="e_scales", tag="e_scales", align_bytes=64)
+            t["e_codes"] = soft.tile([P, QUAD * PASSES * P], U32, name="e_codes", tag="e_codes", align_bytes=64)
+            t["e_scales"] = soft.tile([P, QUAD * PASSES * P], U8, name="e_scales", tag="e_scales", align_bytes=64)
             nc.vector.quantize_mx(
-                out=t["e_codes", s][:].bitcast(FP8X4), scales=t["e_scales", s][:], in_=t["e_grouped", s][:]
+                out=t["e_codes"][:].bitcast(FP8X4),
+                scales=t["e_scales"][:],
+                in_=t["e_grouped", quad][:].rearrange("p r s -> p (r s)"),
             )
 
-        def multiply_context(m, s):
+        def multiply_context(m, quad):
             t = head[m]
             b, h = divmod(m, NH)
-            per_bank = BANK // D
-            if s % per_bank == 0:
-                t["ctx", s // per_bank] = context.tile([P, per_bank, D], F32, name="ctx", tag="ctx")
-            for g in range(PASSES):
-                nc.tensor.matmul_mx(
-                    out=t["ctx", s // per_bank][:, s % per_bank, :],
-                    lhsT=t["e_codes", s][:, g * P : (g + 1) * P].bitcast(FP8X4),
-                    lhsT_scale=t["e_scales", s][:, g * P : (g + 1) * P],
-                    rhs=v_codes[b][:, g, h * D : (h + 1) * D].bitcast(FP8X4),
-                    rhs_scale=v_scales[b][:, g, h * D : (h + 1) * D],
-                    start=(g == 0),
-                    stop=(g == PASSES - 1),
-                )
+            t["ctx", quad] = context.tile([P, QUAD, D], F32, name="ctx", tag="ctx")
+            for r in range(QUAD):
+                for g in range(PASSES):
+                    cols = slice((r * PASSES + g) * P, (r * PASSES + g + 1) * P)
+                    nc.tensor.matmul_mx(
+                        out=t["ctx", quad][:, r, :],
+                        lhsT=t["e_codes"][:, cols].bitcast(FP8X4),
+                        lhsT_scale=t["e_scales"][:, cols],
+                        rhs=v_codes[b][:, g, h * D : (h + 1) * D].bitcast(FP8X4),
+                        rhs_scale=v_scales[b][:, g, h * D : (h + 1) * D],
+                        start=(g == 0),
+                        stop=(g == PASSES - 1),
+                    )
 
         def invert_sums(m):
             t = head[m]
@@ -366,12 +370,11 @@ def tile_adaptiveattention_pa_t_kernel(tc, q, k, value, Wv, bv, scoring_weights,
         def write_out(m):
             t = head[m]
             b, h = divmod(m, NH)
-            per_bank = BANK // D
             o_sb = result.tile([P, TILES, D], F32, name="o_sb", tag="o_sb")
             for s in range(TILES):
                 nc.scalar.activation(
                     out=o_sb[:, s, :],
-                    in_=t["ctx", s // per_bank][:, s % per_bank, :],
+                    in_=t["ctx", s // QUAD][:, s % QUAD, :],
                     func=ACT.Copy,
                     scale=t["sum_inv"][:, s : s + 1],
                 )
@@ -379,103 +382,109 @@ def tile_adaptiveattention_pa_t_kernel(tc, q, k, value, Wv, bv, scoring_weights,
                 out=out[b].rearrange("(p t) c -> p t c", t=TILES)[:, :, h * D : (h + 1) * D], in_=o_sb[:]
             )
 
-        def part_a(m):
-            nxt = m + 1
-            if m + 5 < HEADS:
-                load_head(m + 5)
-            if m + 3 < HEADS:
-                square_head(m + 3)
-            if m >= 0:
-                head[m]["row_sum"] = result.tile([P, TILES], F32, name="row_sum", tag="row_sum")
-            for s in range(TILES + 2):
-                if nxt < HEADS and s < TILES:
-                    if s + 1 < TILES:
-                        multiply_scores(nxt, s + 1)
-                    distance_and_cosine(nxt, s)
-                    floor_distance(nxt, s)
-                if m >= 0:
-                    for w in range(2 * s, min(2 * s + 2, TILES)):
-                        exponential(m, w)
-                        turn_weights(m, w)
-                        if w >= 1:
-                            group_weights(m, w - 1)
-                    if 2 * s == TILES:
-                        group_weights(m, TILES - 1)
-                    if s >= 2:
-                        quantise_weights(m, s - 2)
-                        multiply_context(m, s - 2)
-            if m + 3 < HEADS:
-                sum_squares(m + 3)
+        def period(p):
+            a, b, c = p, p - 1, p - 2
+            has_a, has_b, has_c = a < HEADS, 0 <= b < HEADS, 0 <= c
+            if a + 3 < HEADS:
+                load_head(a + 3)
+            if has_b:
+                floor_distance(b, TILES - 1)
+            for slot in range(TILES):
+                if has_a and slot + 1 < TILES:
+                    multiply_scores(a, slot + 1)
+                elif slot + 1 == TILES and a + 1 < HEADS:
+                    multiply_scores(a + 1, 0)
+                if slot == 1 and a + 1 < HEADS:
+                    sum_squares(a + 1)
+                if has_b:
+                    for s in ROOTS[slot]:
+                        root_distance(b, s)
+                    for s in MIXES[slot]:
+                        mix(b, s)
+                if has_a:
+                    distance_and_cosine(a, slot)
+                if slot == 0 and has_c:
+                    quantise_weights(c, 1)
+                    multiply_context(c, 1)
+                    invert_sums(c)
+                if slot == 1 and a + 1 < HEADS:
+                    floor_norms(a + 1)
+                if has_b:
+                    for s in MAXIMA[slot]:
+                        row_maximum(b, s)
+                if slot == 2:
+                    if a + 1 < HEADS:
+                        root_norms(a + 1)
+                        invert_norms(a + 1)
+                        row_terms(a + 1)
+                    if has_c:
+                        write_out(c)
+                    if a + 2 < HEADS:
+                        turn_head(a + 2, "q")
+                        turn_head(a + 2, "k")
+                if slot == 3:
+                    if a + 1 < HEADS:
+                        spread_key_terms(a + 1)
+                    if has_b:
+                        shift_of(b, 0)
+                        shift_of(b, 1)
+                if has_b:
+                    for s in EXPONENTIALS[slot]:
+                        exponential(b, s)
+                        turn_weights(b, s)
+                        if s >= 1:
+                            group_weights(b, s - 1)
+                        if s + 2 < TILES:
+                            shift_of(b, s + 2)
+                if slot == 6 and has_b:
+                    quantise_weights(b, 0)
+                    multiply_context(b, 0)
+                if slot == 7 and has_b:
+                    group_weights(b, TILES - 1)
+                if has_a:
+                    for s in FLOORS[slot]:
+                        floor_distance(a, s)
+                if slot == 6 and a + 2 < HEADS:
+                    square_head(a + 2)
 
-        def part_b(m):
-            nxt = m + 1
-            if m >= 0:
-                invert_sums(m)
-            if m + 2 < HEADS:
-                row_terms(m + 2)
-                spread_key_terms(m + 2)
-            if nxt < HEADS:
-                for s in range(TILES):
-                    root_distance(nxt, s)
-                    if s < GPSIMD_TILES:
-                        mix(nxt, s)
-            if m >= 0:
-                write_out(m)
-            if m + 2 < HEADS:
-                for n_bank in range(2 * HALVES):
-                    keep_key_terms(m + 2, n_bank)
-            if m + 4 < HEADS:
-                turn_head(m + 4, "q")
-                turn_head(m + 4, "k")
-            if nxt < HEADS:
-                head[nxt]["z_max"] = result.tile([P, TILES], F32, name="z_max", tag="z_max")
-                for s in range(GPSIMD_TILES, TILES):
-                    mix(nxt, s)
-                    row_maximum(nxt, s)
-            if m + 3 < HEADS:
-                floor_norms(m + 3)
-                root_norms(m + 3)
-            if nxt < HEADS:
-                for s in range(GPSIMD_TILES):
-                    row_maximum(nxt, s)
-                t = head[nxt]
-                t["shift"] = result.tile([P, TILES], F32, name="shift", tag="shift")
-                nc.vector.scalar_tensor_tensor(
-                    out=t["shift"][:], in0=t["z_max"][:], scalar=-1.0, in1=t["c"][:], op0=ALU.mult, op1=ALU.mult
-                )
-            if m + 2 < HEADS:
-                multiply_scores(m + 2, 0)
-
-        turn_value(0)
-        for m in range(2):
-            turn_head(m, "q")
-            turn_head(m, "k")
-        square_head(0)
-        turn_value(1)
-        project_value(0)
-        x_nats[2] = load_value(2)
-        sum_squares(0)
-        floor_norms(0)
-        root_norms(0)
-        square_head(1)
-        load_head(2)
-        load_head(3)
-        turn_value(2)
-        project_value(1)
-        x_nats[3] = load_value(3)
-        row_terms(0)
-        spread_key_terms(0)
-        for n_bank in range(2 * HALVES):
-            keep_key_terms(0, n_bank)
-        sum_squares(1)
-        floor_norms(1)
-        root_norms(1)
-        turn_head(2, "q")
-        turn_head(2, "k")
-        turn_value(3)
-        project_value(2)
-        project_value(3)
+        with tc.tile_pool(name="vwork", bufs=2) as vwork:
+            w_nat = vwork.tile([P, NH, HID], BF16, name="w_nat", tag="w_nat", bufs=1)
+            nc.sync.dma_start(out=w_nat[:], in_=Wv.rearrange("(t p) c -> p t c", p=P))
+            x_nats = {0: load_value(0)}
+            load_head(0)
+            load_head(1)
+            x_nats[1] = load_value(1)
+            w_grouped = vwork.tile(
+                [P, NH * P * PACK], BF16, name="w_grouped", tag="w_grouped", bufs=1, align_bytes=64
+            )
+            turn_features(w_nat[:], NH, w_grouped[:])
+            w_codes = vwork.tile([P, HID], U32, name="w_codes", tag="w_codes", bufs=1, align_bytes=64)
+            w_scales = vwork.tile([P, HID], U8, name="w_scales", tag="w_scales", bufs=1, align_bytes=64)
+            nc.vector.quantize_mx(out=w_codes[:].bitcast(FP8X4), scales=w_scales[:], in_=w_grouped[:])
+            turn_value(0)
+            for m in range(2):
+                turn_head(m, "q")
+                turn_head(m, "k")
+            square_head(0)
+            turn_value(1)
+            project_value(0)
+            x_nats[2] = load_value(2)
+            sum_squares(0)
+            floor_norms(0)
+            root_norms(0)
+            square_head(1)
+            load_head(2)
+            turn_value(2)
+            project_value(1)
+            x_nats[3] = load_value(3)
+            invert_norms(0)
+            row_terms(0)
+            spread_key_terms(0)
+            turn_value(3)
+            project_value(2)
+            project_value(3)
+        dist = ctx.enter_context(tc.tile_pool(name="dist", bufs=DIST_BUFS))
+        score = ctx.enter_context(tc.tile_pool(name="score", bufs=SCORE_BUFS))
         multiply_scores(0, 0)
-        for m in range(-1, HEADS):
-            part_a(m)
-            part_b(m)
+        for p in range(HEADS + 2):
+            period(p)

@@ -22,12 +22,14 @@ PACK = 4
 K_PASS = P * PACK
 PASSES = S // K_PASS
 D2_EPS = 1e-12
+NORM2_MAX = 3.0e38
 NORM2_MIN = 1e-20
 W1_MIN = 1e-12
 FAR_MIN = -3.0e38
 QUAD = 4
 DIST_BUFS = 12
 SCORE_BUFS = 14
+VECTOR_GROUPS = (2, 6)
 ROOTS = ((0, 1, 2), (3, 4, 5), (6, 7), (), (), (), (), ())
 MIXES = ((0,), (1, 2), (3,), (4, 5), (6, 7), (), (), ())
 MAXIMA = ((), (0,), (1, 2), (3,), (4, 5), (6, 7), (), ())
@@ -42,8 +44,7 @@ def tile_adaptiveattention_pa_t_kernel(tc, q, k, value, Wv, bv, scoring_weights,
         const = ctx.enter_context(tc.tile_pool(name="const", bufs=1))
         vkeep = ctx.enter_context(tc.tile_pool(name="vkeep", bufs=1))
         nat = ctx.enter_context(tc.tile_pool(name="nat", bufs=3))
-        turned = ctx.enter_context(tc.tile_pool(name="turned", bufs=3))
-        squares = ctx.enter_context(tc.tile_pool(name="squares", bufs=1))
+        turned = ctx.enter_context(tc.tile_pool(name="turned", bufs=2))
         terms = ctx.enter_context(tc.tile_pool(name="terms", bufs=5))
         spread = ctx.enter_context(tc.tile_pool(name="spread", bufs=2))
         soft = ctx.enter_context(tc.tile_pool(name="soft", bufs=2))
@@ -57,8 +58,10 @@ def tile_adaptiveattention_pa_t_kernel(tc, q, k, value, Wv, bv, scoring_weights,
         make_identity(nc, ident_bf[:])
         ident_f32 = const.tile([P, P], F32, name="ident_f32")
         make_identity(nc, ident_f32[:])
-        ones = const.tile([P, 2], F32, name="ones")
-        nc.vector.memset(ones[:], 1.0)
+        key_columns = []
+        for n in range(2):
+            key_columns.append(const.tile([P, P], F32, name="key_columns%d" % n))
+            nc.vector.memset(key_columns[n][:], 0.0)
         sw_all = const.tile([P, 3], BF16, name="sw_all")
         nc.sync.dma_start(out=sw_all[:], in_=scoring_weights.partition_broadcast(P))
         bv_all = const.tile([P, HID], BF16, name="bv_all")
@@ -173,31 +176,29 @@ def tile_adaptiveattention_pa_t_kernel(tc, q, k, value, Wv, bv, scoring_weights,
             head[m][name + "T"] = turned.tile([P, S], BF16, name=name + "T", tag=name + "T")
             nc.scalar.copy(out=head[m][name + "T"][:], in_=bank[:])
 
-        def square_head(m):
-            for name in ("q", "k"):
-                sq = squares.tile([P, S], F32, name=name + "_sq", tag=name + "_sq")
-                nc.gpsimd.tensor_tensor(out=sq[:], in0=head[m][name + "T"][:], in1=head[m][name + "T"][:], op=ALU.mult)
-                head[m][name + "_sq"] = sq
-
-        def sum_squares(m):
-            norm2 = flipped.tile([P, 2 * TILES, 2], F32, name="norm2", tag="eT")
+        def square_tile(m, s):
+            t = head[m]
+            if s == 0:
+                t["norm2"] = terms.tile([P, 2 * TILES], F32, name="norm2", tag="norm2")
             for n_op, name in enumerate(("q", "k")):
-                for t in range(TILES):
-                    nc.tensor.matmul(
-                        out=norm2[:, n_op * TILES + t, :],
-                        lhsT=head[m][name + "_sq"][:, t * P : (t + 1) * P],
-                        rhs=ones[:],
-                        start=True,
-                        stop=True,
-                    )
-            head[m]["norm2"] = norm2
+                col = n_op * TILES + s
+                junk = terms.tile([P, D], BF16, name="junk", tag="junk", bufs=2)
+                nc.scalar.activation(
+                    out=junk[:], in_=t[name + "_nat"][:, s, :], func=ACT.Square, accum_out=t["norm2"][:, col : col + 1]
+                )
+
+        def gpsimd_scale(out_, in_, factor, factor2=1.0):
+            nc.gpsimd.tensor_scalar(out=out_, in0=in_, scalar1=factor, scalar2=factor2, op0=ALU.mult, op1=ALU.mult)
 
         def floor_norms(m):
             t = head[m]
-            t["half"] = terms.tile([P, 2 * TILES], F32, name="half", tag="half")
-            nc.vector.tensor_scalar_mul(out=t["half"][:], in0=t["norm2"][:, :, 0], scalar1=0.5)
             t["floored"] = terms.tile([P, 2 * TILES], F32, name="floored", tag="floored")
-            nc.vector.tensor_scalar_max(out=t["floored"][:], in0=t["norm2"][:, :, 0], scalar1=NORM2_MIN)
+            nc.gpsimd.tensor_scalar(
+                out=t["floored"][:], in0=t["norm2"][:], scalar1=NORM2_MAX, scalar2=NORM2_MIN, op0=ALU.min, op1=ALU.max
+            )
+            t["half"] = terms.tile([P, TILES], F32, name="half", tag="half")
+            gpsimd_scale(t["half"][:], t["norm2"][:, 0:TILES], 0.5)
+            gpsimd_scale(key_columns[m % 2][:, 0:TILES], t["norm2"][:, TILES:], 0.5)
 
         def root_norms(m):
             t = head[m]
@@ -206,8 +207,9 @@ def tile_adaptiveattention_pa_t_kernel(tc, q, k, value, Wv, bv, scoring_weights,
 
         def invert_norms(m):
             t = head[m]
-            t["inv"] = terms.tile([P, 2 * TILES], F32, name="inv", tag="inv")
-            nc.vector.reciprocal(out=t["inv"][:], in_=t["norm"][:])
+            t["inv"] = terms.tile([P, TILES], F32, name="inv", tag="inv")
+            nc.vector.reciprocal(out=t["inv"][:], in_=t["norm"][:, 0:TILES])
+            nc.vector.reciprocal(out=key_columns[m % 2][:, TILES : 2 * TILES], in_=t["norm"][:, TILES:])
 
         def row_terms(m):
             t = head[m]
@@ -217,22 +219,23 @@ def tile_adaptiveattention_pa_t_kernel(tc, q, k, value, Wv, bv, scoring_weights,
                 ("root_scale", "floored", root_factor),
             ):
                 t[name] = terms.tile([P, TILES], F32, name=name, tag=name)
-                nc.gpsimd.tensor_scalar(
-                    out=t[name][:], in0=t[source][:, 0:TILES], scalar1=factor[:], scalar2=1.0, op0=ALU.mult, op1=ALU.mult
-                )
+                gpsimd_scale(t[name][:], t[source][:, 0:TILES], factor[:])
 
         def spread_key_terms(m):
             t = head[m]
-            for name, source in (("k_half", "half"), ("k_inv", "inv")):
-                t[name] = spread.tile([P, S], F32, name=name, tag=name)
-                for half in range(HALVES):
-                    bank = flipped.tile([P, BANK], F32, name="spread", tag="eT")
-                    for c in range(BANK // P):
-                        col = TILES + half * (BANK // P) + c
-                        nc.tensor.transpose(
-                            bank[:, c * P : (c + 1) * P], t[source][:, col : col + 1].to_broadcast([P, P]), ident_f32[:]
-                        )
-                    nc.scalar.copy(out=t[name][:, half * BANK : (half + 1) * BANK], in_=bank[:])
+            b, h = divmod(m, NH)
+            bank = flipped.tile([P, P], F32, name="rows", tag="eT")
+            nc.tensor.transpose(bank[:], key_columns[m % 2][:], ident_f32[:])
+            rows = terms.tile([P, P], F32, name="rows", tag="rows", bufs=2)
+            nc.scalar.copy(out=rows[:], in_=bank[:])
+            parked = out[b, 0 : 2 * TILES, h * D : (h + 1) * D]
+            nc.sync.dma_start(out=parked, in_=rows[0 : 2 * TILES, :])
+            t["key_rows"] = spread.tile([P, 2, TILES, P], F32, name="key_rows", tag="key_rows")
+            nc.sync.dma_start(
+                out=t["key_rows"][:].rearrange("p n t j -> p (n t) j"), in_=parked.partition_broadcast(P)
+            )
+            t["k_half"] = t["key_rows"][:, 0, :, :].rearrange("p t j -> p (t j)")
+            t["k_inv"] = t["key_rows"][:, 1, :, :].rearrange("p t j -> p (t j)")
 
         def multiply_scores(m, s):
             t = head[m]
@@ -327,10 +330,11 @@ def tile_adaptiveattention_pa_t_kernel(tc, q, k, value, Wv, bv, scoring_weights,
 
         def group_weights(m, s):
             t = head[m]
+            copy = nc.vector.tensor_copy if s in VECTOR_GROUPS else nc.scalar.copy
             quad, r = divmod(s, QUAD)
             if r == 0:
                 t["e_grouped", quad] = soft.tile([P, QUAD, S], BF16, name="e_grouped", tag="e_grouped", align_bytes=64)
-            nc.scalar.copy(
+            copy(
                 out=t["e_grouped", quad][:, r, :].bitcast(F32).rearrange("p (g i u) -> p g i u", g=PASSES, u=2),
                 in_=t["eT", s][:].rearrange("p (g u) i -> p g i u", u=2),
             )
@@ -394,8 +398,6 @@ def tile_adaptiveattention_pa_t_kernel(tc, q, k, value, Wv, bv, scoring_weights,
                     multiply_scores(a, slot + 1)
                 elif slot + 1 == TILES and a + 1 < HEADS:
                     multiply_scores(a + 1, 0)
-                if slot == 1 and a + 1 < HEADS:
-                    sum_squares(a + 1)
                 if has_b:
                     for s in ROOTS[slot]:
                         root_distance(b, s)
@@ -403,12 +405,13 @@ def tile_adaptiveattention_pa_t_kernel(tc, q, k, value, Wv, bv, scoring_weights,
                         mix(b, s)
                 if has_a:
                     distance_and_cosine(a, slot)
-                if slot == 0 and has_c:
-                    quantise_weights(c, 1)
-                    multiply_context(c, 1)
-                    invert_sums(c)
-                if slot == 1 and a + 1 < HEADS:
-                    floor_norms(a + 1)
+                if slot == 0:
+                    if has_c:
+                        if TILES - 1 in VECTOR_GROUPS:
+                            group_weights(c, TILES - 1)
+                        quantise_weights(c, 1)
+                        multiply_context(c, 1)
+                        invert_sums(c)
                 if has_b:
                     for s in MAXIMA[slot]:
                         row_maximum(b, s)
@@ -417,11 +420,10 @@ def tile_adaptiveattention_pa_t_kernel(tc, q, k, value, Wv, bv, scoring_weights,
                         root_norms(a + 1)
                         invert_norms(a + 1)
                         row_terms(a + 1)
+                        turn_head(a + 1, "q")
+                        turn_head(a + 1, "k")
                     if has_c:
                         write_out(c)
-                    if a + 2 < HEADS:
-                        turn_head(a + 2, "q")
-                        turn_head(a + 2, "k")
                 if slot == 3:
                     if a + 1 < HEADS:
                         spread_key_terms(a + 1)
@@ -432,20 +434,26 @@ def tile_adaptiveattention_pa_t_kernel(tc, q, k, value, Wv, bv, scoring_weights,
                     for s in EXPONENTIALS[slot]:
                         exponential(b, s)
                         turn_weights(b, s)
-                        if s >= 1:
+                        if s >= 1 and s - 1 not in VECTOR_GROUPS:
                             group_weights(b, s - 1)
                         if s + 2 < TILES:
                             shift_of(b, s + 2)
+                if a + 2 < HEADS:
+                    square_tile(a + 2, slot)
+                if has_b:
+                    for s in VECTOR_GROUPS:
+                        if s + 1 < TILES and s + 1 in EXPONENTIALS[slot]:
+                            group_weights(b, s)
                 if slot == 6 and has_b:
                     quantise_weights(b, 0)
                     multiply_context(b, 0)
-                if slot == 7 and has_b:
+                if slot == 7 and has_b and TILES - 1 not in VECTOR_GROUPS:
                     group_weights(b, TILES - 1)
                 if has_a:
                     for s in FLOORS[slot]:
                         floor_distance(a, s)
-                if slot == 6 and a + 2 < HEADS:
-                    square_head(a + 2)
+            if a + 2 < HEADS:
+                floor_norms(a + 2)
 
         with tc.tile_pool(name="vwork", bufs=2) as vwork:
             w_nat = vwork.tile([P, NH, HID], BF16, name="w_nat", tag="w_nat", bufs=1)
@@ -462,24 +470,25 @@ def tile_adaptiveattention_pa_t_kernel(tc, q, k, value, Wv, bv, scoring_weights,
             w_scales = vwork.tile([P, HID], U8, name="w_scales", tag="w_scales", bufs=1, align_bytes=64)
             nc.vector.quantize_mx(out=w_codes[:].bitcast(FP8X4), scales=w_scales[:], in_=w_grouped[:])
             turn_value(0)
-            for m in range(2):
-                turn_head(m, "q")
-                turn_head(m, "k")
-            square_head(0)
+            for s in range(TILES):
+                square_tile(0, s)
+            floor_norms(0)
+            root_norms(0)
+            turn_head(0, "q")
+            turn_head(0, "k")
             turn_value(1)
             project_value(0)
             x_nats[2] = load_value(2)
-            sum_squares(0)
-            floor_norms(0)
-            root_norms(0)
-            square_head(1)
             load_head(2)
-            turn_value(2)
-            project_value(1)
-            x_nats[3] = load_value(3)
             invert_norms(0)
             row_terms(0)
             spread_key_terms(0)
+            for s in range(TILES):
+                square_tile(1, s)
+            floor_norms(1)
+            turn_value(2)
+            project_value(1)
+            x_nats[3] = load_value(3)
             turn_value(3)
             project_value(2)
             project_value(3)

@@ -27,14 +27,14 @@ NORM2_MIN = 1e-20
 W1_MIN = 1e-12
 FAR_MIN = -3.0e38
 QUAD = 4
-DIST_BUFS = 12
-SCORE_BUFS = 14
+DIST_BUFS = 6
+SCORE_BUFS = 7
 VECTOR_GROUPS = (2, 6)
 ROOTS = ((0, 1, 2), (3, 4, 5), (6, 7), (), (), (), (), ())
-MIXES = ((0,), (1, 2), (3,), (4, 5), (6, 7), (), (), ())
-MAXIMA = ((), (0,), (1, 2), (3,), (4, 5), (6, 7), (), ())
+MIXES = ((0,), (1,), (2,), (), (3,), (), (), ())
+MAXIMA = ((), (), (0,), (1,), (2,), (3,), (), ())
 EXPONENTIALS = ((), (), (), (0,), (1, 2), (3, 4), (5, 6), (7,))
-FLOORS = ((), (), (), (), (), (0, 1, 2), (3, 4), (5, 6))
+FLOORS = ((), (), (), (), (), (0,), (1,), (2,))
 FLOPS = 2 * (B * S * HID * HID + 2 * HEADS * S * S * D)
 
 
@@ -253,8 +253,11 @@ def tile_adaptiveattention_pa_t_kernel(tc, q, k, value, Wv, bv, scoring_weights,
 
         def distance_and_cosine(m, s):
             t = head[m]
-            t["far", s] = dist.tile([P, S], F32, name="far_t", tag="far_t")
-            t["near", s] = score.tile([P, S], F32, name="near_t", tag="near_t")
+            if s % 2 == 0:
+                t["far_pair", s // 2] = dist.tile([P, 2, S], F32, name="far_pair", tag="far_pair")
+                t["near_pair", s // 2] = score.tile([P, 2, S], F32, name="near_pair", tag="near_pair")
+            t["far", s] = t["far_pair", s // 2][:, s % 2, :]
+            t["near", s] = t["near_pair", s // 2][:, s % 2, :]
             for half in range(HALVES):
                 cols = slice(half * BANK, (half + 1) * BANK)
                 nc.vector.scalar_tensor_tensor(
@@ -276,8 +279,8 @@ def tile_adaptiveattention_pa_t_kernel(tc, q, k, value, Wv, bv, scoring_weights,
                     op1=ALU.mult,
                 )
 
-        def floor_distance(m, s):
-            far = head[m]["far", s]
+        def floor_distance(m, pair):
+            far = head[m]["far_pair", pair]
             nc.gpsimd.tensor_scalar(
                 out=far[:], in0=far[:], scalar1=-0.5 * D2_EPS, scalar2=FAR_MIN, op0=ALU.min, op1=ALU.max
             )
@@ -288,16 +291,17 @@ def tile_adaptiveattention_pa_t_kernel(tc, q, k, value, Wv, bv, scoring_weights,
                 out=t["far", s][:], in_=t["far", s][:], func=ACT.Sqrt, scale=t["root_scale"][:, s : s + 1]
             )
 
-        def mix(m, s):
+        def mix(m, pair):
             t = head[m]
-            nc.gpsimd.tensor_tensor(out=t["near", s][:], in0=t["near", s][:], in1=t["far", s][:], op=ALU.subtract)
+            near = t["near_pair", pair]
+            nc.gpsimd.tensor_tensor(out=near[:], in0=near[:], in1=t["far_pair", pair][:], op=ALU.subtract)
 
-        def row_maximum(m, s):
+        def row_maximum(m, pair):
             t = head[m]
-            if s == 0:
+            if pair == 0:
                 t["z_max"] = result.tile([P, TILES], F32, name="z_max", tag="z_max")
             nc.vector.tensor_reduce(
-                out=t["z_max"][:, s : s + 1], in_=t["near", s][:], axis=mybir.AxisListType.X, op=ALU.max, negate=True
+                out=t["z_max"][:, 2 * pair : 2 * pair + 2], in_=t["near_pair", pair][:], axis=mybir.AxisListType.X, op=ALU.max, negate=True
             )
 
         def shift_of(m, s):
@@ -392,7 +396,7 @@ def tile_adaptiveattention_pa_t_kernel(tc, q, k, value, Wv, bv, scoring_weights,
             if a + 3 < HEADS:
                 load_head(a + 3)
             if has_b:
-                floor_distance(b, TILES - 1)
+                floor_distance(b, TILES // 2 - 1)
             for slot in range(TILES):
                 if has_a and slot + 1 < TILES:
                     multiply_scores(a, slot + 1)
@@ -401,8 +405,8 @@ def tile_adaptiveattention_pa_t_kernel(tc, q, k, value, Wv, bv, scoring_weights,
                 if has_b:
                     for s in ROOTS[slot]:
                         root_distance(b, s)
-                    for s in MIXES[slot]:
-                        mix(b, s)
+                    for pair in MIXES[slot]:
+                        mix(b, pair)
                 if has_a:
                     distance_and_cosine(a, slot)
                 if slot == 0:
@@ -413,8 +417,8 @@ def tile_adaptiveattention_pa_t_kernel(tc, q, k, value, Wv, bv, scoring_weights,
                         multiply_context(c, 1)
                         invert_sums(c)
                 if has_b:
-                    for s in MAXIMA[slot]:
-                        row_maximum(b, s)
+                    for pair in MAXIMA[slot]:
+                        row_maximum(b, pair)
                 if slot == 2:
                     if a + 1 < HEADS:
                         root_norms(a + 1)
@@ -450,8 +454,8 @@ def tile_adaptiveattention_pa_t_kernel(tc, q, k, value, Wv, bv, scoring_weights,
                 if slot == 7 and has_b and TILES - 1 not in VECTOR_GROUPS:
                     group_weights(b, TILES - 1)
                 if has_a:
-                    for s in FLOORS[slot]:
-                        floor_distance(a, s)
+                    for pair in FLOORS[slot]:
+                        floor_distance(a, pair)
             if a + 2 < HEADS:
                 floor_norms(a + 2)
 

@@ -22,19 +22,22 @@ PACK = 4
 K_PASS = P * PACK
 PASSES = S // K_PASS
 D2_EPS = 1e-12
-NORM2_MAX = 3.0e38
 NORM2_MIN = 1e-20
 W1_MIN = 1e-12
+TENSOR_TILE = TILES - 1
+ROOT_MAX = 3.0e38
 FAR_MIN = -3.0e38
 QUAD = 4
 DIST_BUFS = 6
 SCORE_BUFS = 7
 VECTOR_GROUPS = (2, 6)
+QUANTISE_SLOT = 0
 ROOTS = ((0, 1, 2), (3, 4, 5), (6, 7), (), (), (), (), ())
-MIXES = ((0,), (1,), (2,), (), (3,), (), (), ())
-MAXIMA = ((), (), (0,), (1,), (2,), (3,), (), ())
+MIXES = (((0, 2),), ((2, 2),), ((4, 2),), ((6, 1), (7, 1)), (), (), (), ())
+MAXIMA = ((), (), ((0, 2),), ((2, 2),), ((4, 2),), ((6, 1), (7, 1)), (), ())
 EXPONENTIALS = ((), (), (), (0,), (1, 2), (3, 4), (5, 6), (7,))
-FLOORS = ((), (), (), (), (), (0,), (1,), (2,))
+FLOORS = ((), (), (), (), (), ((0, 2),), ((2, 2),), ())
+LATE_FLOORS = ((4, 2), (6, 1))
 FLOPS = 2 * (B * S * HID * HID + 2 * HEADS * S * S * D)
 
 
@@ -58,10 +61,12 @@ def tile_adaptiveattention_pa_t_kernel(tc, q, k, value, Wv, bv, scoring_weights,
         make_identity(nc, ident_bf[:])
         ident_f32 = const.tile([P, P], F32, name="ident_f32")
         make_identity(nc, ident_f32[:])
-        key_columns = []
-        for n in range(2):
-            key_columns.append(const.tile([P, P], F32, name="key_columns%d" % n))
-            nc.vector.memset(key_columns[n][:], 0.0)
+        columns = []
+        for n in range(3):
+            columns.append(const.tile([P, P], F32, name="columns%d" % n))
+            nc.vector.memset(columns[n][:], 0.0)
+        norm2_min = const.tile([P, 1], F32, name="norm2_min")
+        nc.vector.memset(norm2_min[:], NORM2_MIN)
         sw_all = const.tile([P, 3], BF16, name="sw_all")
         nc.sync.dma_start(out=sw_all[:], in_=scoring_weights.partition_broadcast(P))
         bv_all = const.tile([P, HID], BF16, name="bv_all")
@@ -136,38 +141,46 @@ def tile_adaptiveattention_pa_t_kernel(tc, q, k, value, Wv, bv, scoring_weights,
             )
             turn_features(x_nats[b][:], PASSES * PACK, x_grouped[b][:])
 
-        def project_value(b):
-            x_codes = vwork.tile([P, PASSES * PACK * P], U32, name="x_codes", tag="x_codes", align_bytes=64)
-            x_scales = vwork.tile([P, PASSES * PACK * P], U8, name="x_scales", tag="x_scales", align_bytes=64)
-            nc.vector.quantize_mx(out=x_codes[:].bitcast(FP8X4), scales=x_scales[:], in_=x_grouped[b][:])
+        x_codes = {}
+        x_scales = {}
+        v_grouped = {}
+
+        def quantise_value(b):
+            x_codes[b] = vwork.tile([P, PASSES * PACK * P], U32, name="x_codes", tag="x_codes", align_bytes=64)
+            x_scales[b] = vwork.tile([P, PASSES * PACK * P], U8, name="x_scales", tag="x_scales", align_bytes=64)
+            nc.vector.quantize_mx(out=x_codes[b][:].bitcast(FP8X4), scales=x_scales[b][:], in_=x_grouped[b][:])
             v_codes[b] = vkeep.tile([P, PASSES, HID], U32, name="v_codes%d" % b, align_bytes=64)
             v_scales[b] = vkeep.tile([P, PASSES, HID], U8, name="v_scales%d" % b, align_bytes=64)
-            for g in range(PASSES):
-                v_grouped = vwork.tile([P, NH, D, PACK], BF16, name="v_grouped", tag="v_grouped", align_bytes=64)
-                for h in range(NH):
-                    vp = banks.tile([P, PACK, D], F32, name="vp", tag="bank")
-                    for t in range(PACK):
-                        rows = slice((g * PACK + t) * P, (g * PACK + t + 1) * P)
-                        nc.tensor.matmul_mx(
-                            out=vp[:, t, :],
-                            lhsT=x_codes[:, rows].bitcast(FP8X4),
-                            lhsT_scale=x_scales[:, rows],
-                            rhs=w_codes[:, h * D : (h + 1) * D].bitcast(FP8X4),
-                            rhs_scale=w_scales[:, h * D : (h + 1) * D],
-                            start=True,
-                            stop=True,
-                        )
-                    nc.vector.tensor_tensor(
-                        out=v_grouped[:, h, :, :],
-                        in0=vp[:].rearrange("p t d -> p d t"),
-                        in1=bv_all[:, h * D : (h + 1) * D].unsqueeze(2).to_broadcast([P, D, PACK]),
-                        op=ALU.add,
+
+        def project_value(b, g):
+            v_grouped[b, g] = vwork.tile([P, NH, D, PACK], BF16, name="v_grouped", tag="v_grouped", align_bytes=64)
+            for h in range(NH):
+                vp = banks.tile([P, PACK, D], F32, name="vp", tag="bank")
+                for t in range(PACK):
+                    rows = slice((g * PACK + t) * P, (g * PACK + t + 1) * P)
+                    nc.tensor.matmul_mx(
+                        out=vp[:, t, :],
+                        lhsT=x_codes[b][:, rows].bitcast(FP8X4),
+                        lhsT_scale=x_scales[b][:, rows],
+                        rhs=w_codes[:, h * D : (h + 1) * D].bitcast(FP8X4),
+                        rhs_scale=w_scales[:, h * D : (h + 1) * D],
+                        start=True,
+                        stop=True,
                     )
-                nc.vector.quantize_mx(
-                    out=v_codes[b][:, g, :].bitcast(FP8X4),
-                    scales=v_scales[b][:, g, :],
-                    in_=v_grouped[:].rearrange("p h d t -> p (h d t)"),
+                nc.vector.tensor_tensor(
+                    out=v_grouped[b, g][:, h, :, :],
+                    in0=vp[:].rearrange("p t d -> p d t"),
+                    in1=bv_all[:, h * D : (h + 1) * D].unsqueeze(2).to_broadcast([P, D, PACK]),
+                    op=ALU.add,
                 )
+
+        def quantise_v(b, g):
+            nc.vector.quantize_mx(
+                out=v_codes[b][:, g, :].bitcast(FP8X4),
+                scales=v_scales[b][:, g, :],
+                in_=v_grouped[b, g][:].rearrange("p h d t -> p (h d t)"),
+            )
+
 
         def turn_head(m, name):
             bank = flipped.tile([P, S], BF16, name="turn", tag="eT")
@@ -187,18 +200,16 @@ def tile_adaptiveattention_pa_t_kernel(tc, q, k, value, Wv, bv, scoring_weights,
                     out=junk[:], in_=t[name + "_nat"][:, s, :], func=ACT.Square, accum_out=t["norm2"][:, col : col + 1]
                 )
 
-        def gpsimd_scale(out_, in_, factor, factor2=1.0):
-            nc.gpsimd.tensor_scalar(out=out_, in0=in_, scalar1=factor, scalar2=factor2, op0=ALU.mult, op1=ALU.mult)
+        def scale_column(m, name, source, factor):
+            head[m][name] = terms.tile([P, source.shape[1]], F32, name=name, tag=name)
+            nc.scalar.activation(out=head[m][name][:], in_=source, func=ACT.Copy, scale=factor)
 
-        def floor_norms(m):
+        def halve_norms(m):
             t = head[m]
             t["floored"] = terms.tile([P, 2 * TILES], F32, name="floored", tag="floored")
-            nc.gpsimd.tensor_scalar(
-                out=t["floored"][:], in0=t["norm2"][:], scalar1=NORM2_MAX, scalar2=NORM2_MIN, op0=ALU.min, op1=ALU.max
-            )
-            t["half"] = terms.tile([P, TILES], F32, name="half", tag="half")
-            gpsimd_scale(t["half"][:], t["norm2"][:, 0:TILES], 0.5)
-            gpsimd_scale(key_columns[m % 2][:, 0:TILES], t["norm2"][:, TILES:], 0.5)
+            nc.scalar.activation(out=t["floored"][:], in_=t["norm2"][:], func=ACT.Identity, bias=norm2_min[:])
+            t["minus_half"] = columns[m % 3][:, 0 : 2 * TILES]
+            nc.scalar.activation(out=t["minus_half"], in_=t["norm2"][:], func=ACT.Copy, scale=-0.5)
 
         def root_norms(m):
             t = head[m]
@@ -207,34 +218,35 @@ def tile_adaptiveattention_pa_t_kernel(tc, q, k, value, Wv, bv, scoring_weights,
 
         def invert_norms(m):
             t = head[m]
-            t["inv"] = terms.tile([P, TILES], F32, name="inv", tag="inv")
-            nc.vector.reciprocal(out=t["inv"][:], in_=t["norm"][:, 0:TILES])
-            nc.vector.reciprocal(out=key_columns[m % 2][:, TILES : 2 * TILES], in_=t["norm"][:, TILES:])
+            t["inv"] = columns[m % 3][:, 2 * TILES : 4 * TILES]
+            nc.vector.reciprocal(out=t["inv"], in_=t["norm"][:])
 
         def row_terms(m):
             t = head[m]
-            for name, source, factor in (
-                ("c", "inv", w1),
-                ("g", "norm", w0_over_w1),
-                ("root_scale", "floored", root_factor),
-            ):
-                t[name] = terms.tile([P, TILES], F32, name=name, tag=name)
-                gpsimd_scale(t[name][:], t[source][:, 0:TILES], factor[:])
+            scale_column(m, "root_scale", t["floored"][:, 0:TILES], root_factor[:])
+            scale_column(m, "g", t["norm"][:, 0:TILES], w0_over_w1[:])
+            col = slice(TENSOR_TILE, TENSOR_TILE + 1)
+            scale_column(m, "root_bias", t["minus_half"][:, col], t["root_scale"][:, col])
+
+        def row_scale(m):
+            scale_column(m, "c", head[m]["inv"][:, 0:TILES], w1[:])
 
         def spread_key_terms(m):
             t = head[m]
             b, h = divmod(m, NH)
             bank = flipped.tile([P, P], F32, name="rows", tag="eT")
-            nc.tensor.transpose(bank[:], key_columns[m % 2][:], ident_f32[:])
+            nc.tensor.transpose(bank[:], columns[m % 3][:], ident_f32[:])
             rows = terms.tile([P, P], F32, name="rows", tag="rows", bufs=2)
             nc.scalar.copy(out=rows[:], in_=bank[:])
             parked = out[b, 0 : 2 * TILES, h * D : (h + 1) * D]
-            nc.sync.dma_start(out=parked, in_=rows[0 : 2 * TILES, :])
+            for n in range(2):
+                source = slice((2 * n + 1) * TILES, (2 * n + 2) * TILES)
+                nc.sync.dma_start(out=parked[n * TILES : (n + 1) * TILES, :], in_=rows[source, :])
             t["key_rows"] = spread.tile([P, 2, TILES, P], F32, name="key_rows", tag="key_rows")
             nc.sync.dma_start(
                 out=t["key_rows"][:].rearrange("p n t j -> p (n t) j"), in_=parked.partition_broadcast(P)
             )
-            t["k_half"] = t["key_rows"][:, 0, :, :].rearrange("p t j -> p (t j)")
+            t["k_minus_half"] = t["key_rows"][:, 0, :, :].rearrange("p t j -> p (t j)")
             t["k_inv"] = t["key_rows"][:, 1, :, :].rearrange("p t j -> p (t j)")
 
         def multiply_scores(m, s):
@@ -258,16 +270,17 @@ def tile_adaptiveattention_pa_t_kernel(tc, q, k, value, Wv, bv, scoring_weights,
                 t["near_pair", s // 2] = score.tile([P, 2, S], F32, name="near_pair", tag="near_pair")
             t["far", s] = t["far_pair", s // 2][:, s % 2, :]
             t["near", s] = t["near_pair", s // 2][:, s % 2, :]
-            for half in range(HALVES):
-                cols = slice(half * BANK, (half + 1) * BANK)
-                nc.vector.scalar_tensor_tensor(
-                    out=t["far", s][:, cols],
-                    in0=t["dot", s][half][:],
-                    scalar=t["half"][:, s : s + 1],
-                    in1=t["k_half"][:, cols],
-                    op0=ALU.subtract,
-                    op1=ALU.subtract,
-                )
+            if s != TENSOR_TILE:
+                for half in range(HALVES):
+                    cols = slice(half * BANK, (half + 1) * BANK)
+                    nc.vector.scalar_tensor_tensor(
+                        out=t["far", s][:, cols],
+                        in0=t["dot", s][half][:],
+                        scalar=t["minus_half"][:, s : s + 1],
+                        in1=t["k_minus_half"][:, cols],
+                        op0=ALU.add,
+                        op1=ALU.add,
+                    )
             for half in range(HALVES):
                 cols = slice(half * BANK, (half + 1) * BANK)
                 nc.vector.scalar_tensor_tensor(
@@ -279,29 +292,64 @@ def tile_adaptiveattention_pa_t_kernel(tc, q, k, value, Wv, bv, scoring_weights,
                     op1=ALU.mult,
                 )
 
-        def floor_distance(m, pair):
-            far = head[m]["far_pair", pair]
+        def run_of(t, name, first, count):
+            return t[name + "_pair", first // 2][:, first % 2 : first % 2 + count, :]
+
+        def floor_distance(m, first, count):
+            far = run_of(head[m], "far", first, count)
             nc.gpsimd.tensor_scalar(
-                out=far[:], in0=far[:], scalar1=-0.5 * D2_EPS, scalar2=FAR_MIN, op0=ALU.min, op1=ALU.max
+                out=far, in0=far, scalar1=-0.5 * D2_EPS, scalar2=FAR_MIN, op0=ALU.min, op1=ALU.max
             )
 
         def root_distance(m, s):
             t = head[m]
+            if s == TENSOR_TILE:
+                for half in range(HALVES):
+                    cols = slice(half * BANK, (half + 1) * BANK)
+                    bank = flipped.tile([P, BANK], F32, name="shifted", tag="eT")
+                    nc.tensor.matmul(
+                        out=bank[:], lhsT=t["qT"][:, s * P : (s + 1) * P], rhs=t["kT"][:, cols], start=True, stop=False
+                    )
+                    for c in range(BANK // P):
+                        col = half * (BANK // P) + c
+                        nc.tensor.matmul(
+                            out=bank[:, c * P : (c + 1) * P],
+                            lhsT=t["minus_half"][:, TILES + col : TILES + col + 1].to_broadcast([P, P]),
+                            rhs=ident_f32[:],
+                            is_transpose=True,
+                            start=False,
+                            stop=(c == BANK // P - 1),
+                        )
+                    nc.scalar.activation(
+                        out=t["far", s][:, cols],
+                        in_=bank[:],
+                        func=ACT.Sqrt,
+                        scale=t["root_scale"][:, s : s + 1],
+                        bias=t["root_bias"][:],
+                    )
+                return
             nc.scalar.activation(
                 out=t["far", s][:], in_=t["far", s][:], func=ACT.Sqrt, scale=t["root_scale"][:, s : s + 1]
             )
 
-        def mix(m, pair):
-            t = head[m]
-            near = t["near_pair", pair]
-            nc.gpsimd.tensor_tensor(out=near[:], in0=near[:], in1=t["far_pair", pair][:], op=ALU.subtract)
+        def guard_root(m, s):
+            far = head[m]["far", s]
+            nc.gpsimd.tensor_scalar(
+                out=far[:], in0=far[:], scalar1=ROOT_MAX, scalar2=0.0, op0=ALU.min, op1=ALU.max
+            )
 
-        def row_maximum(m, pair):
+        def mix(m, first, count):
             t = head[m]
-            if pair == 0:
+            near = run_of(t, "near", first, count)
+            engine = nc.vector if m == HEADS - 1 else nc.gpsimd
+            engine.tensor_tensor(out=near, in0=near, in1=run_of(t, "far", first, count), op=ALU.subtract)
+
+        def row_maximum(m, first, count):
+            t = head[m]
+            if first == 0:
                 t["z_max"] = result.tile([P, TILES], F32, name="z_max", tag="z_max")
             nc.vector.tensor_reduce(
-                out=t["z_max"][:, 2 * pair : 2 * pair + 2], in_=t["near_pair", pair][:], axis=mybir.AxisListType.X, op=ALU.max, negate=True
+                out=t["z_max"][:, first : first + count], in_=run_of(t, "near", first, count), axis=mybir.AxisListType.X, op=ALU.max, negate=True
             )
 
         def shift_of(m, s):
@@ -332,9 +380,12 @@ def tile_adaptiveattention_pa_t_kernel(tc, q, k, value, Wv, bv, scoring_weights,
             for a in range(PASSES * 2):
                 nc.tensor.transpose(t["eT", s][:, a, :], words[:, a * P : (a + 1) * P], ident_f32[:])
 
+        def vector_groups(m):
+            return range(TILES) if m == HEADS - 1 else VECTOR_GROUPS
+
         def group_weights(m, s):
             t = head[m]
-            copy = nc.vector.tensor_copy if s in VECTOR_GROUPS else nc.scalar.copy
+            copy = nc.vector.tensor_copy if s in vector_groups(m) else nc.scalar.copy
             quad, r = divmod(s, QUAD)
             if r == 0:
                 t["e_grouped", quad] = soft.tile([P, QUAD, S], BF16, name="e_grouped", tag="e_grouped", align_bytes=64)
@@ -396,29 +447,34 @@ def tile_adaptiveattention_pa_t_kernel(tc, q, k, value, Wv, bv, scoring_weights,
             if a + 3 < HEADS:
                 load_head(a + 3)
             if has_b:
-                floor_distance(b, TILES // 2 - 1)
+                for run in LATE_FLOORS:
+                    floor_distance(b, *run)
             for slot in range(TILES):
                 if has_a and slot + 1 < TILES:
                     multiply_scores(a, slot + 1)
                 elif slot + 1 == TILES and a + 1 < HEADS:
                     multiply_scores(a + 1, 0)
+                if slot == 1 and a + 1 < HEADS:
+                    halve_norms(a + 1)
+                if slot == 0 and has_c:
+                    group_weights(c, TILES - 1)
                 if has_b:
                     for s in ROOTS[slot]:
                         root_distance(b, s)
-                    for pair in MIXES[slot]:
-                        mix(b, pair)
+                    for run in MIXES[slot]:
+                        if TENSOR_TILE - 1 in run:
+                            guard_root(b, TENSOR_TILE)
+                        mix(b, *run)
                 if has_a:
                     distance_and_cosine(a, slot)
-                if slot == 0:
-                    if has_c:
-                        if TILES - 1 in VECTOR_GROUPS:
-                            group_weights(c, TILES - 1)
-                        quantise_weights(c, 1)
-                        multiply_context(c, 1)
-                        invert_sums(c)
+                if slot == QUANTISE_SLOT and has_c:
+                    for quad in range(TILES // QUAD):
+                        quantise_weights(c, quad)
+                        multiply_context(c, quad)
+                    invert_sums(c)
                 if has_b:
-                    for pair in MAXIMA[slot]:
-                        row_maximum(b, pair)
+                    for run in MAXIMA[slot]:
+                        row_maximum(b, *run)
                 if slot == 2:
                     if a + 1 < HEADS:
                         root_norms(a + 1)
@@ -430,6 +486,7 @@ def tile_adaptiveattention_pa_t_kernel(tc, q, k, value, Wv, bv, scoring_weights,
                         write_out(c)
                 if slot == 3:
                     if a + 1 < HEADS:
+                        row_scale(a + 1)
                         spread_key_terms(a + 1)
                     if has_b:
                         shift_of(b, 0)
@@ -438,26 +495,19 @@ def tile_adaptiveattention_pa_t_kernel(tc, q, k, value, Wv, bv, scoring_weights,
                     for s in EXPONENTIALS[slot]:
                         exponential(b, s)
                         turn_weights(b, s)
-                        if s >= 1 and s - 1 not in VECTOR_GROUPS:
+                        if s >= 1 and s - 1 not in vector_groups(b):
                             group_weights(b, s - 1)
                         if s + 2 < TILES:
                             shift_of(b, s + 2)
                 if a + 2 < HEADS:
                     square_tile(a + 2, slot)
                 if has_b:
-                    for s in VECTOR_GROUPS:
+                    for s in vector_groups(b):
                         if s + 1 < TILES and s + 1 in EXPONENTIALS[slot]:
                             group_weights(b, s)
-                if slot == 6 and has_b:
-                    quantise_weights(b, 0)
-                    multiply_context(b, 0)
-                if slot == 7 and has_b and TILES - 1 not in VECTOR_GROUPS:
-                    group_weights(b, TILES - 1)
                 if has_a:
-                    for pair in FLOORS[slot]:
-                        floor_distance(a, pair)
-            if a + 2 < HEADS:
-                floor_norms(a + 2)
+                    for run in FLOORS[slot]:
+                        floor_distance(a, *run)
 
         with tc.tile_pool(name="vwork", bufs=2) as vwork:
             w_nat = vwork.tile([P, NH, HID], BF16, name="w_nat", tag="w_nat", bufs=1)
@@ -474,28 +524,44 @@ def tile_adaptiveattention_pa_t_kernel(tc, q, k, value, Wv, bv, scoring_weights,
             w_scales = vwork.tile([P, HID], U8, name="w_scales", tag="w_scales", bufs=1, align_bytes=64)
             nc.vector.quantize_mx(out=w_codes[:].bitcast(FP8X4), scales=w_scales[:], in_=w_grouped[:])
             turn_value(0)
+            quantise_value(0)
+            turn_value(1)
+            project_value(0, 0)
+            x_nats[2] = load_value(2)
+            load_head(2)
             for s in range(TILES):
                 square_tile(0, s)
-            floor_norms(0)
+            halve_norms(0)
+            quantise_value(1)
+            project_value(0, 1)
+            quantise_v(0, 0)
             root_norms(0)
             turn_head(0, "q")
             turn_head(0, "k")
-            turn_value(1)
-            project_value(0)
-            x_nats[2] = load_value(2)
-            load_head(2)
+            turn_value(2)
+            x_nats[3] = load_value(3)
+            project_value(1, 0)
+            quantise_v(0, 1)
             invert_norms(0)
             row_terms(0)
+            row_scale(0)
             spread_key_terms(0)
+            quantise_value(2)
+            project_value(1, 1)
+            quantise_v(1, 0)
+            turn_value(3)
             for s in range(TILES):
                 square_tile(1, s)
-            floor_norms(1)
-            turn_value(2)
-            project_value(1)
-            x_nats[3] = load_value(3)
-            turn_value(3)
-            project_value(2)
-            project_value(3)
+            project_value(2, 0)
+            quantise_v(1, 1)
+            quantise_value(3)
+            project_value(2, 1)
+            quantise_v(2, 0)
+            project_value(3, 0)
+            quantise_v(2, 1)
+            project_value(3, 1)
+            quantise_v(3, 0)
+            quantise_v(3, 1)
         dist = ctx.enter_context(tc.tile_pool(name="dist", bufs=DIST_BUFS))
         score = ctx.enter_context(tc.tile_pool(name="score", bufs=SCORE_BUFS))
         multiply_scores(0, 0)

@@ -32,6 +32,17 @@ DIST_BUFS = 6
 SCORE_BUFS = 7
 VECTOR_GROUPS = (2, 6)
 QUANTISE_SLOT = 0
+HALVE_SLOT = 1
+SUMS = (
+    (),
+    (),
+    (),
+    (("q", range(0, 3)),),
+    (("q", range(3, 6)),),
+    (("q", range(6, 8)), ("k", range(0, 2))),
+    (("k", range(2, 5)),),
+    (("k", range(5, 8)),),
+)
 ROOTS = ((0, 1, 2), (3, 4, 5), (6, 7), (), (), (), (), ())
 MIXES = (((0, 2),), ((2, 2),), ((4, 2),), ((6, 1), (7, 1)), (), (), (), ())
 MAXIMA = ((), (), ((0, 2),), ((2, 2),), ((4, 2),), ((6, 1), (7, 1)), (), ())
@@ -46,8 +57,9 @@ def tile_adaptiveattention_pa_t_kernel(tc, q, k, value, Wv, bv, scoring_weights,
     with ExitStack() as ctx:
         const = ctx.enter_context(tc.tile_pool(name="const", bufs=1))
         vkeep = ctx.enter_context(tc.tile_pool(name="vkeep", bufs=1))
-        nat = ctx.enter_context(tc.tile_pool(name="nat", bufs=3))
-        turned = ctx.enter_context(tc.tile_pool(name="turned", bufs=2))
+        nat = ctx.enter_context(tc.tile_pool(name="nat", bufs=2))
+        turned = ctx.enter_context(tc.tile_pool(name="turned", bufs=3))
+        squares = ctx.enter_context(tc.tile_pool(name="squares", bufs=1))
         terms = ctx.enter_context(tc.tile_pool(name="terms", bufs=5))
         spread = ctx.enter_context(tc.tile_pool(name="spread", bufs=2))
         soft = ctx.enter_context(tc.tile_pool(name="soft", bufs=2))
@@ -65,6 +77,8 @@ def tile_adaptiveattention_pa_t_kernel(tc, q, k, value, Wv, bv, scoring_weights,
         for n in range(3):
             columns.append(const.tile([P, P], F32, name="columns%d" % n))
             nc.vector.memset(columns[n][:], 0.0)
+        ones = const.tile([P, 2], F32, name="ones")
+        nc.vector.memset(ones[:], 1.0)
         norm2_min = const.tile([P, 1], F32, name="norm2_min")
         nc.vector.memset(norm2_min[:], NORM2_MIN)
         sw_all = const.tile([P, 3], BF16, name="sw_all")
@@ -186,19 +200,38 @@ def tile_adaptiveattention_pa_t_kernel(tc, q, k, value, Wv, bv, scoring_weights,
             bank = flipped.tile([P, S], BF16, name="turn", tag="eT")
             for t in range(TILES):
                 nc.tensor.transpose(bank[:, t * P : (t + 1) * P], head[m][name + "_nat"][:, t, :], ident_bf[:])
-            head[m][name + "T"] = turned.tile([P, S], BF16, name=name + "T", tag=name + "T")
-            nc.scalar.copy(out=head[m][name + "T"][:], in_=bank[:])
+            turned_ = turned.tile([P, S], BF16, name=name + "T", tag=name + "T")
+            head[m][name + "T"] = turned_
+            nc.scalar.copy(out=turned_[:], in_=bank[:])
+            if "norm2" not in head[m]:
+                head[m][name + "_sq"] = squares.tile([P, S], F32, name=name + "_sq", tag=name + "_sq")
+                nc.scalar.activation(out=head[m][name + "_sq"][:], in_=bank[:], func=ACT.Square)
 
-        def square_tile(m, s):
+        def sum_squares(m, tiles, name):
             t = head[m]
-            if s == 0:
-                t["norm2"] = terms.tile([P, 2 * TILES], F32, name="norm2", tag="norm2")
-            for n_op, name in enumerate(("q", "k")):
-                col = n_op * TILES + s
-                junk = terms.tile([P, D], BF16, name="junk", tag="junk", bufs=2)
-                nc.scalar.activation(
-                    out=junk[:], in_=t[name + "_nat"][:, s, :], func=ACT.Square, accum_out=t["norm2"][:, col : col + 1]
+            if name == "q" and tiles.start == 0:
+                t["sums"] = context.tile([P, 2 * TILES, 2], F32, name="sums", tag="ctx")
+                t["norm2"] = t["sums"][:, :, 0]
+            for s in tiles:
+                nc.tensor.matmul(
+                    out=t["sums"][:, (TILES if name == "k" else 0) + s, :],
+                    lhsT=t[name + "_sq"][:, s * P : (s + 1) * P],
+                    rhs=ones[:],
+                    start=True,
+                    stop=True,
                 )
+
+        def square_tiles(m):
+            t = head[m]
+            norm2 = terms.tile([P, 2 * TILES], F32, name="norm2", tag="norm2", bufs=2)
+            t["norm2"] = norm2[:]
+            for n_op, name in enumerate(("q", "k")):
+                for s in range(TILES):
+                    col = n_op * TILES + s
+                    junk = terms.tile([P, D], BF16, name="junk", tag="junk", bufs=2)
+                    nc.scalar.activation(
+                        out=junk[:], in_=t[name + "_nat"][:, s, :], func=ACT.Square, accum_out=norm2[:, col : col + 1]
+                    )
 
         def scale_column(m, name, source, factor):
             head[m][name] = terms.tile([P, source.shape[1]], F32, name=name, tag=name)
@@ -207,9 +240,9 @@ def tile_adaptiveattention_pa_t_kernel(tc, q, k, value, Wv, bv, scoring_weights,
         def halve_norms(m):
             t = head[m]
             t["floored"] = terms.tile([P, 2 * TILES], F32, name="floored", tag="floored")
-            nc.scalar.activation(out=t["floored"][:], in_=t["norm2"][:], func=ACT.Identity, bias=norm2_min[:])
+            nc.scalar.activation(out=t["floored"][:], in_=t["norm2"], func=ACT.Identity, bias=norm2_min[:])
             t["minus_half"] = columns[m % 3][:, 0 : 2 * TILES]
-            nc.scalar.activation(out=t["minus_half"], in_=t["norm2"][:], func=ACT.Copy, scale=-0.5)
+            nc.scalar.activation(out=t["minus_half"], in_=t["norm2"], func=ACT.Copy, scale=-0.5)
 
         def root_norms(m):
             t = head[m]
@@ -387,7 +420,7 @@ def tile_adaptiveattention_pa_t_kernel(tc, q, k, value, Wv, bv, scoring_weights,
             t = head[m]
             copy = nc.vector.tensor_copy if s in vector_groups(m) else nc.scalar.copy
             quad, r = divmod(s, QUAD)
-            if r == 0:
+            if ("e_grouped", quad) not in t:
                 t["e_grouped", quad] = soft.tile([P, QUAD, S], BF16, name="e_grouped", tag="e_grouped", align_bytes=64)
             copy(
                 out=t["e_grouped", quad][:, r, :].bitcast(F32).rearrange("p (g i u) -> p g i u", g=PASSES, u=2),
@@ -454,19 +487,21 @@ def tile_adaptiveattention_pa_t_kernel(tc, q, k, value, Wv, bv, scoring_weights,
                     multiply_scores(a, slot + 1)
                 elif slot + 1 == TILES and a + 1 < HEADS:
                     multiply_scores(a + 1, 0)
-                if slot == 1 and a + 1 < HEADS:
+                if slot == HALVE_SLOT and a + 1 < HEADS:
                     halve_norms(a + 1)
-                if slot == 0 and has_c:
-                    group_weights(c, TILES - 1)
                 if has_b:
                     for s in ROOTS[slot]:
                         root_distance(b, s)
+                        if s == 0 and has_c:
+                            group_weights(c, TILES - 1)
                     for run in MIXES[slot]:
                         if TENSOR_TILE - 1 in run:
                             guard_root(b, TENSOR_TILE)
                         mix(b, *run)
                 if has_a:
                     distance_and_cosine(a, slot)
+                if slot == 0 and has_c and not has_b:
+                    group_weights(c, TILES - 1)
                 if slot == QUANTISE_SLOT and has_c:
                     for quad in range(TILES // QUAD):
                         quantise_weights(c, quad)
@@ -480,8 +515,9 @@ def tile_adaptiveattention_pa_t_kernel(tc, q, k, value, Wv, bv, scoring_weights,
                         root_norms(a + 1)
                         invert_norms(a + 1)
                         row_terms(a + 1)
-                        turn_head(a + 1, "q")
-                        turn_head(a + 1, "k")
+                    if a + 2 < HEADS:
+                        turn_head(a + 2, "q")
+                        turn_head(a + 2, "k")
                     if has_c:
                         write_out(c)
                 if slot == 3:
@@ -500,7 +536,8 @@ def tile_adaptiveattention_pa_t_kernel(tc, q, k, value, Wv, bv, scoring_weights,
                         if s + 2 < TILES:
                             shift_of(b, s + 2)
                 if a + 2 < HEADS:
-                    square_tile(a + 2, slot)
+                    for name, tiles in SUMS[slot]:
+                        sum_squares(a + 2, tiles, name)
                 if has_b:
                     for s in vector_groups(b):
                         if s + 1 < TILES and s + 1 in EXPONENTIALS[slot]:
@@ -529,8 +566,7 @@ def tile_adaptiveattention_pa_t_kernel(tc, q, k, value, Wv, bv, scoring_weights,
             project_value(0, 0)
             x_nats[2] = load_value(2)
             load_head(2)
-            for s in range(TILES):
-                square_tile(0, s)
+            square_tiles(0)
             halve_norms(0)
             quantise_value(1)
             project_value(0, 1)
@@ -550,8 +586,9 @@ def tile_adaptiveattention_pa_t_kernel(tc, q, k, value, Wv, bv, scoring_weights,
             project_value(1, 1)
             quantise_v(1, 0)
             turn_value(3)
-            for s in range(TILES):
-                square_tile(1, s)
+            square_tiles(1)
+            turn_head(1, "q")
+            turn_head(1, "k")
             project_value(2, 0)
             quantise_v(1, 1)
             quantise_value(3)

@@ -32,6 +32,9 @@ DIST_BUFS = 6
 SCORE_BUFS = 7
 VECTOR_GROUPS = (2, 6)
 QUANTISE_SLOT = 0
+SHIFT_SLOT = 1
+VECTOR_OUT = (0,)
+OUT_SLOT = 2
 HALVE_SLOT = 1
 SUMS = (
     (),
@@ -334,28 +337,37 @@ def tile_adaptiveattention_pa_t_kernel(tc, q, k, value, Wv, bv, scoring_weights,
                 out=far, in0=far, scalar1=-0.5 * D2_EPS, scalar2=FAR_MIN, op0=ALU.min, op1=ALU.max
             )
 
+        def shift_scores(m):
+            t = head[m]
+            t["shifted"] = []
+            for half in range(HALVES):
+                bank = flipped.tile([P, BANK], F32, name="shifted", tag="eT")
+                nc.tensor.matmul(
+                    out=bank[:],
+                    lhsT=t["qT"][:, TENSOR_TILE * P : (TENSOR_TILE + 1) * P],
+                    rhs=t["kT"][:, half * BANK : (half + 1) * BANK],
+                    start=True,
+                    stop=False,
+                )
+                for c in range(BANK // P):
+                    col = TILES + half * (BANK // P) + c
+                    nc.tensor.matmul(
+                        out=bank[:, c * P : (c + 1) * P],
+                        lhsT=t["minus_half"][:, col : col + 1].to_broadcast([P, P]),
+                        rhs=ident_f32[:],
+                        is_transpose=True,
+                        start=False,
+                        stop=(c == BANK // P - 1),
+                    )
+                t["shifted"].append(bank)
+
         def root_distance(m, s):
             t = head[m]
             if s == TENSOR_TILE:
                 for half in range(HALVES):
-                    cols = slice(half * BANK, (half + 1) * BANK)
-                    bank = flipped.tile([P, BANK], F32, name="shifted", tag="eT")
-                    nc.tensor.matmul(
-                        out=bank[:], lhsT=t["qT"][:, s * P : (s + 1) * P], rhs=t["kT"][:, cols], start=True, stop=False
-                    )
-                    for c in range(BANK // P):
-                        col = half * (BANK // P) + c
-                        nc.tensor.matmul(
-                            out=bank[:, c * P : (c + 1) * P],
-                            lhsT=t["minus_half"][:, TILES + col : TILES + col + 1].to_broadcast([P, P]),
-                            rhs=ident_f32[:],
-                            is_transpose=True,
-                            start=False,
-                            stop=(c == BANK // P - 1),
-                        )
                     nc.scalar.activation(
-                        out=t["far", s][:, cols],
-                        in_=bank[:],
+                        out=t["far", s][:, half * BANK : (half + 1) * BANK],
+                        in_=t["shifted"][half][:],
                         func=ACT.Sqrt,
                         scale=t["root_scale"][:, s : s + 1],
                         bias=t["root_bias"][:],
@@ -463,13 +475,23 @@ def tile_adaptiveattention_pa_t_kernel(tc, q, k, value, Wv, bv, scoring_weights,
             t = head[m]
             b, h = divmod(m, NH)
             o_sb = result.tile([P, TILES, D], F32, name="o_sb", tag="o_sb")
-            for s in range(TILES):
-                nc.scalar.activation(
-                    out=o_sb[:, s, :],
-                    in_=t["ctx", s // QUAD][:, s % QUAD, :],
-                    func=ACT.Copy,
-                    scale=t["sum_inv"][:, s : s + 1],
-                )
+            for quad in range(TILES // QUAD):
+                tiles = range(quad * QUAD, (quad + 1) * QUAD)
+                if quad in VECTOR_OUT:
+                    nc.vector.tensor_tensor(
+                        out=o_sb[:, tiles.start : tiles.stop, :],
+                        in0=t["ctx", quad][:],
+                        in1=t["sum_inv"][:, tiles.start : tiles.stop].unsqueeze(2).to_broadcast([P, QUAD, D]),
+                        op=ALU.mult,
+                    )
+                    continue
+                for s in tiles:
+                    nc.scalar.activation(
+                        out=o_sb[:, s, :],
+                        in_=t["ctx", quad][:, s % QUAD, :],
+                        func=ACT.Copy,
+                        scale=t["sum_inv"][:, s : s + 1],
+                    )
             nc.sync.dma_start(
                 out=out[b].rearrange("(p t) c -> p t c", t=TILES)[:, :, h * D : (h + 1) * D], in_=o_sb[:]
             )
@@ -483,6 +505,8 @@ def tile_adaptiveattention_pa_t_kernel(tc, q, k, value, Wv, bv, scoring_weights,
                 for run in LATE_FLOORS:
                     floor_distance(b, *run)
             for slot in range(TILES):
+                if slot == SHIFT_SLOT and has_b:
+                    shift_scores(b)
                 if has_a and slot + 1 < TILES:
                     multiply_scores(a, slot + 1)
                 elif slot + 1 == TILES and a + 1 < HEADS:
@@ -518,8 +542,8 @@ def tile_adaptiveattention_pa_t_kernel(tc, q, k, value, Wv, bv, scoring_weights,
                     if a + 2 < HEADS:
                         turn_head(a + 2, "q")
                         turn_head(a + 2, "k")
-                    if has_c:
-                        write_out(c)
+                if slot == OUT_SLOT and has_c:
+                    write_out(c)
                 if slot == 3:
                     if a + 1 < HEADS:
                         row_scale(a + 1)

@@ -87,7 +87,6 @@ def tile_adaptiveattention_pa_t_kernel(tc, q, k, value, Wv, bv, scoring_weights,
         sw_all = const.tile([P, 3], BF16, name="sw_all")
         nc.sync.dma_start(out=sw_all[:], in_=scoring_weights.partition_broadcast(P))
         bv_all = const.tile([P, HID], BF16, name="bv_all")
-        nc.sync.dma_start(out=bv_all[:], in_=bv.partition_broadcast(P))
 
         head = {}
 
@@ -101,10 +100,11 @@ def tile_adaptiveattention_pa_t_kernel(tc, q, k, value, Wv, bv, scoring_weights,
 
         def load_value(b):
             x_nat = vwork.tile([P, PASSES * PACK, HID], BF16, name="x_nat", tag="x_nat")
-            nc.sync.dma_start(
-                out=x_nat[:].rearrange("p (a e) c -> p a (e c)", e=2),
-                in_=value[b].rearrange("(a p e) c -> p a (e c)", p=P, e=2),
-            )
+            for g in range(PASSES):
+                nc.sync.dma_start(
+                    out=x_nat[:, g * PACK : (g + 1) * PACK, :].rearrange("p (a e) c -> p a (e c)", e=2),
+                    in_=value[b, g * K_PASS : (g + 1) * K_PASS].rearrange("(a p e) c -> p a (e c)", p=P, e=2),
+                )
             return x_nat
 
         sw = const.tile([P, 3], F32, name="sw")
@@ -426,7 +426,7 @@ def tile_adaptiveattention_pa_t_kernel(tc, q, k, value, Wv, bv, scoring_weights,
                 nc.tensor.transpose(t["eT", s][:, a, :], words[:, a * P : (a + 1) * P], ident_f32[:])
 
         def vector_groups(m):
-            return range(TILES) if m == HEADS - 1 else VECTOR_GROUPS
+            return (2, 6) if m == HEADS - 1 else VECTOR_GROUPS
 
         def group_weights(m, s):
             t = head[m]
@@ -484,17 +484,18 @@ def tile_adaptiveattention_pa_t_kernel(tc, q, k, value, Wv, bv, scoring_weights,
                         in1=t["sum_inv"][:, tiles.start : tiles.stop].unsqueeze(2).to_broadcast([P, QUAD, D]),
                         op=ALU.mult,
                     )
-                    continue
-                for s in tiles:
-                    nc.scalar.activation(
-                        out=o_sb[:, s, :],
-                        in_=t["ctx", quad][:, s % QUAD, :],
-                        func=ACT.Copy,
-                        scale=t["sum_inv"][:, s : s + 1],
-                    )
-            nc.sync.dma_start(
-                out=out[b].rearrange("(p t) c -> p t c", t=TILES)[:, :, h * D : (h + 1) * D], in_=o_sb[:]
-            )
+                else:
+                    for s in tiles:
+                        nc.scalar.activation(
+                            out=o_sb[:, s, :],
+                            in_=t["ctx", quad][:, s % QUAD, :],
+                            func=ACT.Copy,
+                            scale=t["sum_inv"][:, s : s + 1],
+                        )
+                nc.sync.dma_start(
+                    out=out[b].rearrange("(p t) c -> p t c", t=TILES)[:, tiles.start : tiles.stop, h * D : (h + 1) * D],
+                    in_=o_sb[:, tiles.start : tiles.stop, :],
+                )
 
         def period(p):
             a, b, c = p, p - 1, p - 2
@@ -522,16 +523,19 @@ def tile_adaptiveattention_pa_t_kernel(tc, q, k, value, Wv, bv, scoring_weights,
                         if TENSOR_TILE - 1 in run:
                             guard_root(b, TENSOR_TILE)
                         mix(b, *run)
+                        if b == HEADS - 1:
+                            row_maximum(b, *run)
                 if has_a:
                     distance_and_cosine(a, slot)
                 if slot == 0 and has_c and not has_b:
                     group_weights(c, TILES - 1)
                 if slot == QUANTISE_SLOT and has_c:
                     for quad in range(TILES // QUAD):
-                        quantise_weights(c, quad)
-                        multiply_context(c, quad)
+                        if quad > 0 or c < HEADS - 1:
+                            quantise_weights(c, quad)
+                            multiply_context(c, quad)
                     invert_sums(c)
-                if has_b:
+                if has_b and b < HEADS - 1:
                     for run in MAXIMA[slot]:
                         row_maximum(b, *run)
                 if slot == 2:
@@ -566,6 +570,9 @@ def tile_adaptiveattention_pa_t_kernel(tc, q, k, value, Wv, bv, scoring_weights,
                     for s in vector_groups(b):
                         if s + 1 < TILES and s + 1 in EXPONENTIALS[slot]:
                             group_weights(b, s)
+                if slot == 6 and b == HEADS - 1:
+                    quantise_weights(b, 0)
+                    multiply_context(b, 0)
                 if has_a:
                     for run in FLOORS[slot]:
                         floor_distance(a, *run)
@@ -575,6 +582,7 @@ def tile_adaptiveattention_pa_t_kernel(tc, q, k, value, Wv, bv, scoring_weights,
             nc.sync.dma_start(out=w_nat[:], in_=Wv.rearrange("(t p) c -> p t c", p=P))
             x_nats = {0: load_value(0)}
             load_head(0)
+            nc.sync.dma_start(out=bv_all[:], in_=bv.partition_broadcast(P))
             load_head(1)
             x_nats[1] = load_value(1)
             w_grouped = vwork.tile(

from contextlib import ExitStack

import concourse.mybir as mybir
from concourse.masks import make_identity

F32 = mybir.dt.float32
BF16 = mybir.dt.bfloat16
U32 = mybir.dt.uint32
U8 = mybir.dt.uint8
FP8X4 = mybir.dt.float8_e4m3fn_x4
ALU = mybir.AluOpType
ACT = mybir.ActivationFunctionType

P = 128
B, NH, S, D = 4, 4, 1024, 128
HID = NH * D
HEADS = B * NH
TILES = S // P
BANK = 512
HALVES = S // BANK
PACK = 4
K_PASS = P * PACK
PASSES = S // K_PASS
D2_EPS = 1e-12
NORM2_MIN = 1e-20
W1_MIN = 1e-12
TENSOR_TILE = TILES - 1
ROOT_MAX = 3.0e38
FAR_MIN = -3.0e38
QUAD = 4
DIST_BUFS = 6
SCORE_BUFS = 7
VECTOR_GROUPS = (2, 6)
QUANTISE_SLOT = 0
SHIFT_SLOT = 1
VECTOR_OUT = (0,)
OUT_SLOT = 2
HALVE_SLOT = 1
SUMS = (
    (),
    (),
    (),
    (("q", range(0, 3)),),
    (("q", range(3, 6)),),
    (("q", range(6, 8)), ("k", range(0, 2))),
    (("k", range(2, 5)),),
    (("k", range(5, 8)),),
)
ROOTS = ((0, 1, 2), (3, 4, 5), (6, 7), (), (), (), (), ())
MIXES = (((0, 2),), ((2, 2),), ((4, 2),), ((6, 1), (7, 1)), (), (), (), ())
MAXIMA = ((), (), ((0, 2),), ((2, 2),), ((4, 2),), ((6, 1), (7, 1)), (), ())
EXPONENTIALS = ((), (), (), (0,), (1, 2), (3, 4), (5, 6), (7,))
FLOORS = ((), (), (), (), (), ((0, 2),), ((2, 2),), ())
LATE_FLOORS = ((4, 2), (6, 1))
FLOPS = 2 * (B * S * HID * HID + 2 * HEADS * S * S * D)


def tile_adaptiveattention_pa_t_kernel(tc, q, k, value, Wv, bv, scoring_weights, out):
    nc = tc.nc
    with ExitStack() as ctx:
        const = ctx.enter_context(tc.tile_pool(name="const", bufs=1))
        vkeep = ctx.enter_context(tc.tile_pool(name="vkeep", bufs=1))
        nat = ctx.enter_context(tc.tile_pool(name="nat", bufs=2))
        turned = ctx.enter_context(tc.tile_pool(name="turned", bufs=3))
        squares = ctx.enter_context(tc.tile_pool(name="squares", bufs=1))
        terms = ctx.enter_context(tc.tile_pool(name="terms", bufs=5))
        spread = ctx.enter_context(tc.tile_pool(name="spread", bufs=2))
        soft = ctx.enter_context(tc.tile_pool(name="soft", bufs=2))
        result = ctx.enter_context(tc.tile_pool(name="result", bufs=2))
        banks = ctx.enter_context(tc.psum_pool(name="banks", bufs=4))
        flipped = ctx.enter_context(tc.psum_pool(name="flipped", bufs=2))
        context = ctx.enter_context(tc.psum_pool(name="context", bufs=2))
        ctx.enter_context(tc.manual_schedule())

        ident_bf = const.tile([P, P], BF16, name="ident_bf")
        make_identity(nc, ident_bf[:])
        ident_f32 = const.tile([P, P], F32, name="ident_f32")
        make_identity(nc, ident_f32[:])
        columns = []
        for n in range(3):
            columns.append(const.tile([P, P], F32, name="columns%d" % n))
            nc.vector.memset(columns[n][:], 0.0)
        ones = const.tile([P, 2], F32, name="ones")
        nc.vector.memset(ones[:], 1.0)
        norm2_min = const.tile([P, 1], F32, name="norm2_min")
        nc.vector.memset(norm2_min[:], NORM2_MIN)
        sw_all = const.tile([P, 3], BF16, name="sw_all")
        nc.sync.dma_start(out=sw_all[:], in_=scoring_weights.partition_broadcast(P))
        bv_all = const.tile([P, HID], BF16, name="bv_all")

        head = {}

        def load_head(m):
            b, h = divmod(m, NH)
            q_nat = nat.tile([P, TILES, D], BF16, name="q_nat", tag="q_nat")
            nc.sync.dma_start(out=q_nat[:], in_=q[b, h].rearrange("(p t) d -> p t d", t=TILES))
            k_nat = nat.tile([P, TILES, D], BF16, name="k_nat", tag="k_nat")
            nc.sync.dma_start(out=k_nat[:], in_=k[b, h].rearrange("(t p) d -> p t d", p=P))
            head[m] = {"q_nat": q_nat, "k_nat": k_nat}

        def load_value(b):
            x_nat = vwork.tile([P, PASSES * PACK, HID], BF16, name="x_nat", tag="x_nat")
            for g in range(PASSES):
                nc.sync.dma_start(
                    out=x_nat[:, g * PACK : (g + 1) * PACK, :].rearrange("p (a e) c -> p a (e c)", e=2),
                    in_=value[b, g * K_PASS : (g + 1) * K_PASS].rearrange("(a p e) c -> p a (e c)", p=P, e=2),
                )
            return x_nat

        sw = const.tile([P, 3], F32, name="sw")
        nc.vector.tensor_copy(out=sw[:], in_=sw_all[:])
        sw_max = const.tile([P, 1], F32, name="sw_max")
        nc.vector.tensor_reduce(out=sw_max[:], in_=sw[:], axis=mybir.AxisListType.X, op=ALU.max)
        sw_shift = const.tile([P, 1], F32, name="sw_shift")
        nc.vector.tensor_scalar_mul(out=sw_shift[:], in0=sw_max[:], scalar1=-1.0)
        sw_exp = const.tile([P, 3], F32, name="sw_exp")
        sw_sum = const.tile([P, 1], F32, name="sw_sum")
        nc.scalar.activation(out=sw_exp[:], in_=sw[:], func=ACT.Exp, bias=sw_shift[:], accum_out=sw_sum[:])
        sw_inv = const.tile([P, 1], F32, name="sw_inv")
        nc.vector.reciprocal(out=sw_inv[:], in_=sw_sum[:])
        w_mix = const.tile([P, 3], F32, name="w_mix")
        nc.vector.tensor_scalar_mul(out=w_mix[:], in0=sw_exp[:], scalar1=sw_inv[:])
        w1 = const.tile([P, 1], F32, name="w1")
        nc.vector.tensor_scalar_max(out=w1[:], in0=w_mix[:, 1:2], scalar1=W1_MIN)
        w1_inv = const.tile([P, 1], F32, name="w1_inv")
        nc.vector.reciprocal(out=w1_inv[:], in_=w1[:])
        w0_over_w1 = const.tile([P, 1], F32, name="w0_over_w1")
        nc.vector.tensor_mul(out=w0_over_w1[:], in0=w_mix[:, 0:1], in1=w1_inv[:])
        w2_over_w1 = const.tile([P, 1], F32, name="w2_over_w1")
        nc.vector.tensor_mul(out=w2_over_w1[:], in0=w_mix[:, 2:3], in1=w1_inv[:])
        root_factor = const.tile([P, 1], F32, name="root_factor")
        nc.vector.scalar_tensor_tensor(
            out=root_factor[:], in0=w2_over_w1[:], scalar=-2.0, in1=w2_over_w1[:], op0=ALU.mult, op1=ALU.mult
        )

        def turn_features(rows, n_tiles, grouped):
            words = rows.bitcast(F32)
            grouped_words = grouped.bitcast(F32).rearrange("p (a r u) -> p a r u", r=P, u=2)
            for pair in range(n_tiles // 2):
                bank = banks.tile([P, 2, 2, P], F32, name="feat", tag="bank")
                for a in range(2):
                    for u in range(2):
                        nc.tensor.transpose(
                            bank[:, a, u, :], words[:, 2 * pair + a, u * P : (u + 1) * P], ident_f32[:]
                        )
                nc.scalar.copy(
                    out=grouped_words[:, 2 * pair : 2 * pair + 2, :, :],
                    in_=bank[:].rearrange("p a u r -> p a r u"),
                )

        v_codes = {}
        v_scales = {}
        x_grouped = {}

        def turn_value(b):
            x_grouped[b] = vwork.tile(
                [P, PASSES * PACK * P * PACK], BF16, name="x_grouped", tag="x_grouped", align_bytes=64
            )
            turn_features(x_nats[b][:], PASSES * PACK, x_grouped[b][:])

        x_codes = {}
        x_scales = {}
        v_grouped = {}

        def quantise_value(b):
            x_codes[b] = vwork.tile([P, PASSES * PACK * P], U32, name="x_codes", tag="x_codes", align_bytes=64)
            x_scales[b] = vwork.tile([P, PASSES * PACK * P], U8, name="x_scales", tag="x_scales", align_bytes=64)
            nc.vector.quantize_mx(out=x_codes[b][:].bitcast(FP8X4), scales=x_scales[b][:], in_=x_grouped[b][:])
            v_codes[b] = vkeep.tile([P, PASSES, HID], U32, name="v_codes%d" % b, align_bytes=64)
            v_scales[b] = vkeep.tile([P, PASSES, HID], U8, name="v_scales%d" % b, align_bytes=64)

        def project_value(b, g):
            v_grouped[b, g] = vwork.tile([P, NH, D, PACK], BF16, name="v_grouped", tag="v_grouped", align_bytes=64)
            for h in range(NH):
                vp = banks.tile([P, PACK, D], F32, name="vp", tag="bank")
                for t in range(PACK):
                    rows = slice((g * PACK + t) * P, (g * PACK + t + 1) * P)
                    nc.tensor.matmul_mx(
                        out=vp[:, t, :],
                        lhsT=x_codes[b][:, rows].bitcast(FP8X4),
                        lhsT_scale=x_scales[b][:, rows],
                        rhs=w_codes[:, h * D : (h + 1) * D].bitcast(FP8X4),
                        rhs_scale=w_scales[:, h * D : (h + 1) * D],
                        start=True,
                        stop=True,
                    )
                nc.vector.tensor_tensor(
                    out=v_grouped[b, g][:, h, :, :],
                    in0=vp[:].rearrange("p t d -> p d t"),
                    in1=bv_all[:, h * D : (h + 1) * D].unsqueeze(2).to_broadcast([P, D, PACK]),
                    op=ALU.add,
                )

        def quantise_v(b, g):
            nc.vector.quantize_mx(
                out=v_codes[b][:, g, :].bitcast(FP8X4),
                scales=v_scales[b][:, g, :],
                in_=v_grouped[b, g][:].rearrange("p h d t -> p (h d t)"),
            )


        def turn_head(m, name):
            bank = flipped.tile([P, S], BF16, name="turn", tag="eT")
            for t in range(TILES):
                nc.tensor.transpose(bank[:, t * P : (t + 1) * P], head[m][name + "_nat"][:, t, :], ident_bf[:])
            turned_ = turned.tile([P, S], BF16, name=name + "T", tag=name + "T")
            head[m][name + "T"] = turned_
            nc.scalar.copy(out=turned_[:], in_=bank[:])
            if "norm2" not in head[m]:
                head[m][name + "_sq"] = squares.tile([P, S], F32, name=name + "_sq", tag=name + "_sq")
                nc.scalar.activation(out=head[m][name + "_sq"][:], in_=bank[:], func=ACT.Square)

        def sum_squares(m, tiles, name):
            t = head[m]
            if name == "q" and tiles.start == 0:
                t["sums"] = context.tile([P, 2 * TILES, 2], F32, name="sums", tag="ctx")
                t["norm2"] = t["sums"][:, :, 0]
            for s in tiles:
                nc.tensor.matmul(
                    out=t["sums"][:, (TILES if name == "k" else 0) + s, :],
                    lhsT=t[name + "_sq"][:, s * P : (s + 1) * P],
                    rhs=ones[:],
                    start=True,
                    stop=True,
                )

        def square_tiles(m):
            t = head[m]
            norm2 = terms.tile([P, 2 * TILES], F32, name="norm2", tag="norm2", bufs=2)
            t["norm2"] = norm2[:]
            for n_op, name in enumerate(("q", "k")):
                for s in range(TILES):
                    col = n_op * TILES + s
                    junk = terms.tile([P, D], BF16, name="junk", tag="junk", bufs=2)
                    nc.scalar.activation(
                        out=junk[:], in_=t[name + "_nat"][:, s, :], func=ACT.Square, accum_out=norm2[:, col : col + 1]
                    )

        def scale_column(m, name, source, factor):
            head[m][name] = terms.tile([P, source.shape[1]], F32, name=name, tag=name)
            nc.scalar.activation(out=head[m][name][:], in_=source, func=ACT.Copy, scale=factor)

        def halve_norms(m):
            t = head[m]
            t["floored"] = terms.tile([P, 2 * TILES], F32, name="floored", tag="floored")
            nc.scalar.activation(out=t["floored"][:], in_=t["norm2"], func=ACT.Identity, bias=norm2_min[:])
            t["minus_half"] = columns[m % 3][:, 0 : 2 * TILES]
            nc.scalar.activation(out=t["minus_half"], in_=t["norm2"], func=ACT.Copy, scale=-0.5)

        def root_norms(m):
            t = head[m]
            t["norm"] = terms.tile([P, 2 * TILES], F32, name="norm", tag="norm")
            nc.scalar.activation(out=t["norm"][:], in_=t["floored"][:], func=ACT.Sqrt)

        def invert_norms(m):
            t = head[m]
            t["inv"] = columns[m % 3][:, 2 * TILES : 4 * TILES]
            nc.vector.reciprocal(out=t["inv"], in_=t["norm"][:])

        def row_terms(m):
            t = head[m]
            scale_column(m, "root_scale", t["floored"][:, 0:TILES], root_factor[:])
            scale_column(m, "g", t["norm"][:, 0:TILES], w0_over_w1[:])
            col = slice(TENSOR_TILE, TENSOR_TILE + 1)
            scale_column(m, "root_bias", t["minus_half"][:, col], t["root_scale"][:, col])

        def row_scale(m):
            scale_column(m, "c", head[m]["inv"][:, 0:TILES], w1[:])

        def spread_key_terms(m):
            t = head[m]
            b, h = divmod(m, NH)
            bank = flipped.tile([P, P], F32, name="rows", tag="eT")
            nc.tensor.transpose(bank[:], columns[m % 3][:], ident_f32[:])
            rows = terms.tile([P, P], F32, name="rows", tag="rows", bufs=2)
            nc.scalar.copy(out=rows[:], in_=bank[:])
            parked = out[b, 0 : 2 * TILES, h * D : (h + 1) * D]
            for n in range(2):
                source = slice((2 * n + 1) * TILES, (2 * n + 2) * TILES)
                nc.sync.dma_start(out=parked[n * TILES : (n + 1) * TILES, :], in_=rows[source, :])
            t["key_rows"] = spread.tile([P, 2, TILES, P], F32, name="key_rows", tag="key_rows")
            nc.sync.dma_start(
                out=t["key_rows"][:].rearrange("p n t j -> p (n t) j"), in_=parked.partition_broadcast(P)
            )
            t["k_minus_half"] = t["key_rows"][:, 0, :, :].rearrange("p t j -> p (t j)")
            t["k_inv"] = t["key_rows"][:, 1, :, :].rearrange("p t j -> p (t j)")

        def multiply_scores(m, s):
            t = head[m]
            t["dot", s] = []
            for half in range(HALVES):
                bank = banks.tile([P, BANK], F32, name="dot", tag="bank")
                nc.tensor.matmul(
                    out=bank[:],
                    lhsT=t["qT"][:, s * P : (s + 1) * P],
                    rhs=t["kT"][:, half * BANK : (half + 1) * BANK],
                    start=True,
                    stop=True,
                )
                t["dot", s].append(bank)

        def distance_and_cosine(m, s):
            t = head[m]
            if s % 2 == 0:
                t["far_pair", s // 2] = dist.tile([P, 2, S], F32, name="far_pair", tag="far_pair")
                t["near_pair", s // 2] = score.tile([P, 2, S], F32, name="near_pair", tag="near_pair")
            t["far", s] = t["far_pair", s // 2][:, s % 2, :]
            t["near", s] = t["near_pair", s // 2][:, s % 2, :]
            if s != TENSOR_TILE:
                for half in range(HALVES):
                    cols = slice(half * BANK, (half + 1) * BANK)
                    nc.vector.scalar_tensor_tensor(
                        out=t["far", s][:, cols],
                        in0=t["dot", s][half][:],
                        scalar=t["minus_half"][:, s : s + 1],
                        in1=t["k_minus_half"][:, cols],
                        op0=ALU.add,
                        op1=ALU.add,
                    )
            for half in range(HALVES):
                cols = slice(half * BANK, (half + 1) * BANK)
                nc.vector.scalar_tensor_tensor(
                    out=t["near", s][:, cols],
                    in0=t["k_inv"][:, cols],
                    scalar=t["g"][:, s : s + 1],
                    in1=t["dot", s][half][:],
                    op0=ALU.add,
                    op1=ALU.mult,
                )

        def run_of(t, name, first, count):
            return t[name + "_pair", first // 2][:, first % 2 : first % 2 + count, :]

        def floor_distance(m, first, count):
            far = run_of(head[m], "far", first, count)
            nc.gpsimd.tensor_scalar(
                out=far, in0=far, scalar1=-0.5 * D2_EPS, scalar2=FAR_MIN, op0=ALU.min, op1=ALU.max
            )

        def shift_scores(m):
            t = head[m]
            t["shifted"] = []
            for half in range(HALVES):
                bank = flipped.tile([P, BANK], F32, name="shifted", tag="eT")
                nc.tensor.matmul(
                    out=bank[:],
                    lhsT=t["qT"][:, TENSOR_TILE * P : (TENSOR_TILE + 1) * P],
                    rhs=t["kT"][:, half * BANK : (half + 1) * BANK],
                    start=True,
                    stop=False,
                )
                for c in range(BANK // P):
                    col = TILES + half * (BANK // P) + c
                    nc.tensor.matmul(
                        out=bank[:, c * P : (c + 1) * P],
                        lhsT=t["minus_half"][:, col : col + 1].to_broadcast([P, P]),
                        rhs=ident_f32[:],
                        is_transpose=True,
                        start=False,
                        stop=(c == BANK // P - 1),
                    )
                t["shifted"].append(bank)

        def root_distance(m, s):
            t = head[m]
            if s == TENSOR_TILE:
                for half in range(HALVES):
                    nc.scalar.activation(
                        out=t["far", s][:, half * BANK : (half + 1) * BANK],
                        in_=t["shifted"][half][:],
                        func=ACT.Sqrt,
                        scale=t["root_scale"][:, s : s + 1],
                        bias=t["root_bias"][:],
                    )
                return
            nc.scalar.activation(
                out=t["far", s][:], in_=t["far", s][:], func=ACT.Sqrt, scale=t["root_scale"][:, s : s + 1]
            )

        def guard_root(m, s):
            far = head[m]["far", s]
            nc.gpsimd.tensor_scalar(
                out=far[:], in0=far[:], scalar1=ROOT_MAX, scalar2=0.0, op0=ALU.min, op1=ALU.max
            )

        def mix(m, first, count):
            t = head[m]
            near = run_of(t, "near", first, count)
            engine = nc.vector if m == HEADS - 1 else nc.gpsimd
            engine.tensor_tensor(out=near, in0=near, in1=run_of(t, "far", first, count), op=ALU.subtract)

        def row_maximum(m, first, count):
            t = head[m]
            if first == 0:
                t["z_max"] = result.tile([P, TILES], F32, name="z_max", tag="z_max")
            nc.vector.tensor_reduce(
                out=t["z_max"][:, first : first + count], in_=run_of(t, "near", first, count), axis=mybir.AxisListType.X, op=ALU.max, negate=True
            )

        def shift_of(m, s):
            t = head[m]
            if s == 0:
                t["shift"] = result.tile([P, TILES], F32, name="shift", tag="shift")
                t["row_sum"] = result.tile([P, TILES], F32, name="row_sum", tag="row_sum")
            nc.scalar.activation(
                out=t["shift"][:, s : s + 1], in_=t["z_max"][:, s : s + 1], func=ACT.Copy, scale=t["c"][:, s : s + 1]
            )

        def exponential(m, s):
            t = head[m]
            t["e", s] = soft.tile([P, S], BF16, name="e", tag="e", bufs=3)
            nc.scalar.activation(
                out=t["e", s][:],
                in_=t["near", s][:],
                func=ACT.Exp,
                bias=t["shift"][:, s : s + 1],
                scale=t["c"][:, s : s + 1],
                accum_out=t["row_sum"][:, s : s + 1],
            )

        def turn_weights(m, s):
            t = head[m]
            t["eT", s] = flipped.tile([P, PASSES * 2, P], F32, name="eT", tag="eT")
            words = t["e", s][:].bitcast(F32)
            for a in range(PASSES * 2):
                nc.tensor.transpose(t["eT", s][:, a, :], words[:, a * P : (a + 1) * P], ident_f32[:])

        def vector_groups(m):
            return (2, 6) if m == HEADS - 1 else VECTOR_GROUPS

        def group_weights(m, s):
            t = head[m]
            copy = nc.vector.tensor_copy if s in vector_groups(m) else nc.scalar.copy
            quad, r = divmod(s, QUAD)
            if ("e_grouped", quad) not in t:
                t["e_grouped", quad] = soft.tile([P, QUAD, S], BF16, name="e_grouped", tag="e_grouped", align_bytes=64)
            copy(
                out=t["e_grouped", quad][:, r, :].bitcast(F32).rearrange("p (g i u) -> p g i u", g=PASSES, u=2),
                in_=t["eT", s][:].rearrange("p (g u) i -> p g i u", u=2),
            )

        def quantise_weights(m, quad):
            t = head[m]
            t["e_codes"] = soft.tile([P, QUAD * PASSES * P], U32, name="e_codes", tag="e_codes", align_bytes=64)
            t["e_scales"] = soft.tile([P, QUAD * PASSES * P], U8, name="e_scales", tag="e_scales", align_bytes=64)
            nc.vector.quantize_mx(
                out=t["e_codes"][:].bitcast(FP8X4),
                scales=t["e_scales"][:],
                in_=t["e_grouped", quad][:].rearrange("p r s -> p (r s)"),
            )

        def multiply_context(m, quad):
            t = head[m]
            b, h = divmod(m, NH)
            t["ctx", quad] = context.tile([P, QUAD, D], F32, name="ctx", tag="ctx")
            for r in range(QUAD):
                for g in range(PASSES):
                    cols = slice((r * PASSES + g) * P, (r * PASSES + g + 1) * P)
                    nc.tensor.matmul_mx(
                        out=t["ctx", quad][:, r, :],
                        lhsT=t["e_codes"][:, cols].bitcast(FP8X4),
                        lhsT_scale=t["e_scales"][:, cols],
                        rhs=v_codes[b][:, g, h * D : (h + 1) * D].bitcast(FP8X4),
                        rhs_scale=v_scales[b][:, g, h * D : (h + 1) * D],
                        start=(g == 0),
                        stop=(g == PASSES - 1),
                    )

        def invert_sums(m):
            t = head[m]
            t["sum_inv"] = result.tile([P, TILES], F32, name="sum_inv", tag="sum_inv")
            nc.vector.reciprocal(out=t["sum_inv"][:], in_=t["row_sum"][:])

        def write_out(m):
            t = head[m]
            b, h = divmod(m, NH)
            o_sb = result.tile([P, TILES, D], F32, name="o_sb", tag="o_sb")
            for quad in range(TILES // QUAD):
                tiles = range(quad * QUAD, (quad + 1) * QUAD)
                if quad in VECTOR_OUT:
                    nc.vector.tensor_tensor(
                        out=o_sb[:, tiles.start : tiles.stop, :],
                        in0=t["ctx", quad][:],
                        in1=t["sum_inv"][:, tiles.start : tiles.stop].unsqueeze(2).to_broadcast([P, QUAD, D]),
                        op=ALU.mult,
                    )
                else:
                    for s in tiles:
                        nc.scalar.activation(
                            out=o_sb[:, s, :],
                            in_=t["ctx", quad][:, s % QUAD, :],
                            func=ACT.Copy,
                            scale=t["sum_inv"][:, s : s + 1],
                        )
                nc.sync.dma_start(
                    out=out[b].rearrange("(p t) c -> p t c", t=TILES)[:, tiles.start : tiles.stop, h * D : (h + 1) * D],
                    in_=o_sb[:, tiles.start : tiles.stop, :],
                )

        def period(p):
            a, b, c = p, p - 1, p - 2
            has_a, has_b, has_c = a < HEADS, 0 <= b < HEADS, 0 <= c
            if a + 3 < HEADS:
                load_head(a + 3)
            if has_b:
                for run in LATE_FLOORS:
                    floor_distance(b, *run)
            for slot in range(TILES):
                if slot == SHIFT_SLOT and has_b:
                    shift_scores(b)
                if has_a and slot + 1 < TILES:
                    multiply_scores(a, slot + 1)
                elif slot + 1 == TILES and a + 1 < HEADS:
                    multiply_scores(a + 1, 0)
                if slot == HALVE_SLOT and a + 1 < HEADS:
                    halve_norms(a + 1)
                if has_b:
                    for s in ROOTS[slot]:
                        root_distance(b, s)
                        if s == 0 and has_c:
                            group_weights(c, TILES - 1)
                    for run in MIXES[slot]:
                        if TENSOR_TILE - 1 in run:
                            guard_root(b, TENSOR_TILE)
                        mix(b, *run)
                        if b == HEADS - 1:
                            row_maximum(b, *run)
                if has_a:
                    distance_and_cosine(a, slot)
                if slot == 0 and has_c and not has_b:
                    group_weights(c, TILES - 1)
                if slot == QUANTISE_SLOT and has_c:
                    for quad in range(TILES // QUAD):
                        if quad > 0 or c < HEADS - 1:
                            quantise_weights(c, quad)
                            multiply_context(c, quad)
                    invert_sums(c)
                if has_b and b < HEADS - 1:
                    for run in MAXIMA[slot]:
                        row_maximum(b, *run)
                if slot == 2:
                    if a + 1 < HEADS:
                        root_norms(a + 1)
                        invert_norms(a + 1)
                        row_terms(a + 1)
                    if a + 2 < HEADS:
                        turn_head(a + 2, "q")
                        turn_head(a + 2, "k")
                if slot == OUT_SLOT and has_c:
                    write_out(c)
                if slot == 3:
                    if a + 1 < HEADS:
                        row_scale(a + 1)
                        spread_key_terms(a + 1)
                    if has_b:
                        shift_of(b, 0)
                        shift_of(b, 1)
                if has_b:
                    for s in EXPONENTIALS[slot]:
                        exponential(b, s)
                        turn_weights(b, s)
                        if s >= 1 and s - 1 not in vector_groups(b):
                            group_weights(b, s - 1)
                        if s + 2 < TILES:
                            shift_of(b, s + 2)
                if a + 2 < HEADS:
                    for name, tiles in SUMS[slot]:
                        sum_squares(a + 2, tiles, name)
                if has_b:
                    for s in vector_groups(b):
                        if s + 1 < TILES and s + 1 in EXPONENTIALS[slot]:
                            group_weights(b, s)
                if slot == 6 and b == HEADS - 1:
                    quantise_weights(b, 0)
                    multiply_context(b, 0)
                if has_a:
                    for run in FLOORS[slot]:
                        floor_distance(a, *run)

        with tc.tile_pool(name="vwork", bufs=2) as vwork:
            w_nat = vwork.tile([P, NH, HID], BF16, name="w_nat", tag="w_nat", bufs=1)
            nc.sync.dma_start(out=w_nat[:], in_=Wv.rearrange("(t p) c -> p t c", p=P))
            x_nats = {0: load_value(0)}
            load_head(0)
            nc.sync.dma_start(out=bv_all[:], in_=bv.partition_broadcast(P))
            load_head(1)
            x_nats[1] = load_value(1)
            w_grouped = vwork.tile(
                [P, NH * P * PACK], BF16, name="w_grouped", tag="w_grouped", bufs=1, align_bytes=64
            )
            turn_features(w_nat[:], NH, w_grouped[:])
            w_codes = vwork.tile([P, HID], U32, name="w_codes", tag="w_codes", bufs=1, align_bytes=64)
            w_scales = vwork.tile([P, HID], U8, name="w_scales", tag="w_scales", bufs=1, align_bytes=64)
            nc.vector.quantize_mx(out=w_codes[:].bitcast(FP8X4), scales=w_scales[:], in_=w_grouped[:])
            turn_value(0)
            quantise_value(0)
            turn_value(1)
            project_value(0, 0)
            x_nats[2] = load_value(2)
            load_head(2)
            square_tiles(0)
            halve_norms(0)
            quantise_value(1)
            project_value(0, 1)
            quantise_v(0, 0)
            root_norms(0)
            turn_head(0, "q")
            turn_head(0, "k")
            turn_value(2)
            x_nats[3] = load_value(3)
            project_value(1, 0)
            quantise_v(0, 1)
            invert_norms(0)
            row_terms(0)
            row_scale(0)
            spread_key_terms(0)
            quantise_value(2)
            project_value(1, 1)
            quantise_v(1, 0)
            turn_value(3)
            square_tiles(1)
            turn_head(1, "q")
            turn_head(1, "k")
            project_value(2, 0)
            quantise_v(1, 1)
            quantise_value(3)
            project_value(2, 1)
            quantise_v(2, 0)
            project_value(3, 0)
            quantise_v(2, 1)
            project_value(3, 1)
            quantise_v(3, 0)
            quantise_v(3, 1)
        dist = ctx.enter_context(tc.tile_pool(name="dist", bufs=DIST_BUFS))
        score = ctx.enter_context(tc.tile_pool(name="score", bufs=SCORE_BUFS))
        multiply_scores(0, 0)
        for p in range(HEADS + 2):
            period(p)
